import numpy as np
import ml_dtypes


def mxq(x, axis, fmt="e4m3"):
    dtype, down = {"e4m3": (ml_dtypes.float8_e4m3fn, 7), "e5m2": (ml_dtypes.float8_e5m2, 14)}[fmt]
    v = np.moveaxis(np.asarray(x, np.float32).astype(ml_dtypes.bfloat16).astype(np.float64), axis, -1)
    blocks = v.reshape(v.shape[:-1] + (-1, 32))
    amax = np.abs(blocks).max(-1, keepdims=True)
    byte = np.maximum(np.where(amax > 0, np.frexp(amax)[1] - 1 + 127, 0) - down, 1)
    scale = np.exp2(byte - 127.0)
    codes = (blocks / scale).astype(np.float32).astype(dtype).astype(np.float64)
    return np.moveaxis((codes * scale).reshape(v.shape), -1, axis)


WIDE = False


def mx_kscale(k):
    if not WIDE:
        return np.ones(k)
    levels = np.array([10, -10, 5, -5, 0])
    a = np.random.permutation(np.resize(levels, k // 512 * 4)).reshape(k // 512, 4)
    idx = np.arange(k)
    return np.exp2(a[idx // 512, idx % 128 // 32])


BF16 = ml_dtypes.bfloat16


def bf(x):
    return np.asarray(x, np.float32).astype(BF16)


def f64(x):
    return np.asarray(x).astype(np.float64)


B, V, R = 128, 16384, 512

ALPHA = 0.3


def setup_inputs():
    s = mx_kscale(V)
    return {"logits": bf(np.random.standard_normal((B, V)) * s / s.max()),
            "W": bf(np.random.standard_normal((V, R)) * 2.0 * (B / R) ** 0.25 / s[:, None])}


def reference(logits, W):
    logits, W = f64(logits), f64(W)
    l_n = np.linalg.norm(logits)
    logits_n = logits / l_n
    h = mxq(logits_n, 1, "e4m3") @ mxq(W, 0, "e4m3")
    minted = mxq(h, 1, "e4m3") @ mxq(W, 1, "e4m3").T
    minted = minted / np.linalg.norm(minted)
    out = (1.0 - ALPHA) * minted + ALPHA * logits_n
    out = out / np.linalg.norm(out) * l_n
    return out

@@ -1,0 +1,326 @@
+from contextlib import ExitStack
+
+import concourse.mybir as mybir
+from concourse.masks import make_identity
+
+F32 = mybir.dt.float32
+BF16 = mybir.dt.bfloat16
+U32 = mybir.dt.uint32
+U8 = mybir.dt.uint8
+FP8X4 = mybir.dt.float8_e4m3fn_x4
+ALU = mybir.AluOpType
+ACT = mybir.ActivationFunctionType
+AXIS = mybir.AxisListType
+
+P = 128
+V = 16384
+R = 512
+PACK = 4
+K_PASS = P * PACK
+GROUPS = V // K_PASS
+ALPHA = 0.3
+KEEP = 1.0 - ALPHA
+
+FLOPS = 2 * 2 * P * V * R
+
+PIECE = 4096
+PIECES = V // PIECE
+STATS = 512
+L_CHUNK = 8
+STORE = 2048
+SCALAR_COLS = 224
+
+
+def inverse_root(nc, pool, x, name):
+    root = pool.tile([P, 1], F32, name=name + "_root")
+    nc.scalar.activation(out=root[:], in_=x, func=ACT.Sqrt)
+    rough = pool.tile([P, 1], F32, name=name + "_rough")
+    nc.vector.reciprocal(out=rough[:], in_=root[:])
+    unit = pool.tile([P, 1], F32, name=name + "_unit")
+    nc.vector.tensor_scalar(
+        out=unit[:], in0=rough[:], scalar1=x, scalar2=rough[:, 0:1], op0=ALU.mult, op1=ALU.mult
+    )
+    step = pool.tile([P, 1], F32, name=name + "_step")
+    nc.vector.tensor_scalar(
+        out=step[:], in0=unit[:], scalar1=-0.5, scalar2=1.5, op0=ALU.mult, op1=ALU.add
+    )
+    better = pool.tile([P, 1], F32, name=name)
+    nc.vector.tensor_mul(out=better[:], in0=rough[:], in1=step[:])
+    return better
+
+
+def tile_lowrankredistributor_k_kernel(tc, logits, W, out):
+    nc = tc.nc
+    with ExitStack() as ctx:
+        keep = ctx.enter_context(tc.tile_pool(name="keep", bufs=1))
+        psum = ctx.enter_context(tc.psum_pool(name="psum", bufs=1))
+
+        ident_f32 = keep.tile([P, P], F32)
+        make_identity(nc, ident_f32[:])
+        ident_bf = keep.tile([P, P], BF16)
+        make_identity(nc, ident_bf[:])
+        ones = keep.tile([P, P], F32)
+        nc.vector.memset(ones[:], 1.0)
+        warm = keep.tile([P, 1], F32)
+        nc.vector.memset(warm[:], 1.0)
+        nc.scalar.activation(out=warm[:], in_=warm[:], func=ACT.Sqrt)
+
+        logits_sb = keep.tile([P, V], BF16)
+        wt_codes = keep.tile([P, GROUPS, K_PASS], U32, align_bytes=64)
+        wt_scales = keep.tile([P, GROUPS, K_PASS], U8, align_bytes=64)
+        l_norm = keep.tile([P, 1], F32)
+        h_acc = psum.tile([P, R], F32, tag="h_acc")
+
+        for i in range(PIECES):
+            cols = slice(i * PIECE, (i + 1) * PIECE)
+            nc.sync.dma_start(out=logits_sb[:, cols], in_=logits[:, cols])
+
+        with ExitStack() as first:
+            early = first.enter_context(tc.tile_pool(name="early", bufs=1))
+            stream = first.enter_context(tc.tile_pool(name="stream", bufs=3))
+
+            stats = early.tile([P, V // STATS, 6], F32)
+            for i in range(V // STATS):
+                nc.vector.bn_stats(
+                    out=stats[:, i, :], in_=logits_sb[:, i * STATS : (i + 1) * STATS]
+                )
+
+            lt = early.tile([P, GROUPS, P, PACK], BF16, align_bytes=64)
+            lt_words = (
+                lt[:]
+                .rearrange("p g b t -> p (g b t)")
+                .bitcast(F32)
+                .rearrange("p (g b u) -> p g b u", b=P, u=2)
+            )
+            logit_words = logits_sb[:].bitcast(F32)
+            for pair in range(GROUPS // 2):
+                bank = psum.tile([P, 2, 2, P], F32, tag="bank", bufs=6)
+                for g2 in range(2):
+                    for u in range(2):
+                        w0 = 256 * (2 * pair + g2) + P * u
+                        nc.tensor.transpose(
+                            out=bank[:, g2, u, :],
+                            in_=logit_words[:, w0 : w0 + P],
+                            identity=ident_f32[:],
+                        )
+                nc.scalar.copy(
+                    out=lt_words[:, 2 * pair : 2 * pair + 2, :, :],
+                    in_=bank[:].rearrange("p g u b -> p g b u"),
+                )
+
+            mean_var = early.tile([P, 2], F32)
+            nc.vector.bn_aggr(out=mean_var[:], in_=stats[:].rearrange("p c s -> p (c s)"))
+            sq = early.tile([P, 1], F32)
+            nc.vector.scalar_tensor_tensor(
+                out=sq[:],
+                in0=mean_var[:, 0:1],
+                scalar=mean_var[:, 0:1],
+                in1=mean_var[:, 1:2],
+                op0=ALU.mult,
+                op1=ALU.add,
+            )
+            sq_all = psum.tile([P, 1], F32, tag="small")
+            nc.tensor.matmul(out=sq_all[:], lhsT=ones[:], rhs=sq[:], start=True, stop=True)
+            l_sq = early.tile([P, 1], F32)
+            nc.vector.tensor_scalar(
+                out=l_sq[:], in0=sq_all[:], scalar1=float(V), scalar2=None, op0=ALU.mult
+            )
+            l_inv = inverse_root(nc, keep, l_sq[:, 0:1], "l_inv")
+            nc.vector.tensor_mul(out=l_norm[:], in0=l_sq[:], in1=l_inv[:])
+
+            l_codes = early.tile([P, GROUPS, P], U32, align_bytes=64)
+            l_scales = early.tile([P, GROUPS, P], U8, align_bytes=64)
+            for c in range(GROUPS // L_CHUNK):
+                gs = slice(c * L_CHUNK, (c + 1) * L_CHUNK)
+                chunk = lt[:, gs].rearrange("p g b t -> p (g b t)")
+                nc.vector.tensor_scalar(
+                    out=chunk, in0=chunk, scalar1=l_inv[:, 0:1], scalar2=None, op0=ALU.mult
+                )
+                nc.vector.quantize_mx(
+                    out=l_codes[:, gs, :].rearrange("p g b -> p (g b)").bitcast(FP8X4),
+                    scales=l_scales[:, gs, :].rearrange("p g b -> p (g b)"),
+                    in_=chunk,
+                )
+
+            w_rows = W.rearrange("(c p e) r -> p c (e r)", p=P, e=2)
+            for g in range(GROUPS):
+                raw = stream.tile([P, PACK, R], BF16, tag="raw", bufs=5)
+                nc.sync.dma_start(
+                    out=raw[:].rearrange("p (u e) r -> p u (e r)", e=2),
+                    in_=w_rows[:, 2 * g : 2 * g + 2, :],
+                )
+
+                by_v = stream.tile([P, R, PACK], BF16, tag="by_v", align_bytes=64)
+                nc.scalar.copy(
+                    out=by_v[:, :SCALAR_COLS, :].rearrange("p (c i) t -> p c t i", i=4),
+                    in_=raw[:, :, :SCALAR_COLS].rearrange("p t (c i) -> p c t i", i=4),
+                )
+                nc.vector.tensor_copy(
+                    out=by_v[:, SCALAR_COLS:, :].rearrange("p (c i) t -> p c t i", i=4),
+                    in_=raw[:, :, SCALAR_COLS:].rearrange("p t (c i) -> p c t i", i=4),
+                )
+
+                raw_words = (
+                    raw[:]
+                    .rearrange("p t r -> p (t r)")
+                    .bitcast(F32)
+                    .rearrange("p (t w) -> p t w", t=PACK)
+                )
+                by_r = stream.tile([P, K_PASS, PACK], BF16, tag="by_r", align_bytes=64)
+                by_r_words = (
+                    by_r[:]
+                    .rearrange("q n t -> q (n t)")
+                    .bitcast(F32)
+                    .rearrange("q (a p e u) -> q a p e u", a=2, e=2, u=2)
+                )
+                for a in range(2):
+                    bank = psum.tile([P, 2, 2, P], F32, tag="bank", bufs=6)
+                    for e in range(2):
+                        for u in range(2):
+                            nc.tensor.transpose(
+                                out=bank[:, e, u, :],
+                                in_=raw_words[:, 2 * a + e, P * u : P * u + P],
+                                identity=ident_f32[:],
+                            )
+                    nc.scalar.copy(
+                        out=by_r_words[:, a], in_=bank[:].rearrange("q e u p -> q p e u")
+                    )
+
+                w0_codes = stream.tile([P, R], U32, tag="w0_codes", bufs=4, align_bytes=64)
+                w0_scales = stream.tile([P, R], U8, tag="w0_scales", bufs=4, align_bytes=64)
+                nc.vector.quantize_mx(
+                    out=w0_codes[:].bitcast(FP8X4),
+                    scales=w0_scales[:],
+                    in_=by_v[:].rearrange("p r t -> p (r t)"),
+                )
+                nc.vector.quantize_mx(
+                    out=wt_codes[:, g, :].bitcast(FP8X4),
+                    scales=wt_scales[:, g, :],
+                    in_=by_r[:].rearrange("q n t -> q (n t)"),
+                )
+                nc.tensor.matmul_mx(
+                    out=h_acc[:],
+                    lhsT=l_codes[:, g, :].bitcast(FP8X4),
+                    lhsT_scale=l_scales[:, g, :],
+                    rhs=w0_codes[:].bitcast(FP8X4),
+                    rhs_scale=w0_scales[:],
+                    start=(g == 0),
+                    stop=(g == GROUPS - 1),
+                )
+
+        tail = ctx.enter_context(tc.tile_pool(name="tail", bufs=1))
+
+        h_bf = tail.tile([P, PACK, P], BF16)
+        nc.vector.tensor_copy(
+            out=h_bf[:].rearrange("b (u e) q -> b u e q", e=2),
+            in_=h_acc[:].rearrange("b (u q e) -> b u e q", u=2, e=2),
+        )
+        h_t = psum.tile([P, PACK, P], BF16, tag="small")
+        for t in range(PACK):
+            nc.tensor.transpose(out=h_t[:, t, :], in_=h_bf[:, t, :], identity=ident_bf[:])
+        h_by_r = tail.tile([P, P, PACK], BF16, align_bytes=64)
+        nc.vector.tensor_copy(out=h_by_r[:], in_=h_t[:].rearrange("q t b -> q b t"))
+        h_codes = tail.tile([P, P], U32, align_bytes=64)
+        h_scales = tail.tile([P, P], U8, align_bytes=64)
+        nc.vector.quantize_mx(
+            out=h_codes[:].bitcast(FP8X4),
+            scales=h_scales[:],
+            in_=h_by_r[:].rearrange("q b t -> q (b t)"),
+        )
+
+        def minted_bank(g):
+            bank = psum.tile([P, K_PASS], F32, tag="bank", bufs=6)
+            nc.tensor.matmul_mx(
+                out=bank[:],
+                lhsT=h_codes[:].bitcast(FP8X4),
+                lhsT_scale=h_scales[:],
+                rhs=wt_codes[:, g, :].bitcast(FP8X4),
+                rhs_scale=wt_scales[:, g, :],
+                start=True,
+                stop=True,
+            )
+            return bank
+
+        mm_parts = tail.tile([P, GROUPS], F32)
+        ml_parts = tail.tile([P, GROUPS], F32)
+        for g in range(GROUPS):
+            cols = slice(g * K_PASS, (g + 1) * K_PASS)
+            bank = minted_bank(g)
+            junk_s = tail.tile([P, K_PASS], BF16, tag="junk_s", bufs=4)
+            nc.scalar.activation(
+                out=junk_s[:], in_=bank[:], func=ACT.Square, accum_out=mm_parts[:, g : g + 1]
+            )
+            junk_v = tail.tile([P, K_PASS], F32, tag="junk_v", bufs=4)
+            nc.vector.scalar_tensor_tensor(
+                out=junk_v[:],
+                in0=bank[:],
+                scalar=1.0,
+                in1=logits_sb[:, cols],
+                op0=ALU.mult,
+                op1=ALU.mult,
+                accum_out=ml_parts[:, g : g + 1],
+            )
+
+        sums = tail.tile([P, 2], F32)
+        nc.vector.tensor_reduce(out=sums[:, 0:1], in_=mm_parts[:], axis=AXIS.X, op=ALU.add)
+        nc.vector.tensor_reduce(out=sums[:, 1:2], in_=ml_parts[:], axis=AXIS.X, op=ALU.add)
+        sums_all = psum.tile([P, 2], F32, tag="small")
+        nc.tensor.matmul(out=sums_all[:], lhsT=ones[:], rhs=sums[:], start=True, stop=True)
+        totals = tail.tile([P, 2], F32)
+        nc.vector.tensor_copy(out=totals[:], in_=sums_all[:])
+        m_inv = inverse_root(nc, tail, totals[:, 0:1], "m_inv")
+        both_inv = tail.tile([P, 1], F32)
+        nc.vector.tensor_scalar(
+            out=both_inv[:],
+            in0=m_inv[:],
+            scalar1=l_inv[:, 0:1],
+            scalar2=2.0 * KEEP * ALPHA,
+            op0=ALU.mult,
+            op1=ALU.mult,
+        )
+        o_sq = tail.tile([P, 1], F32)
+        nc.vector.tensor_scalar(
+            out=o_sq[:],
+            in0=totals[:, 1:2],
+            scalar1=both_inv[:, 0:1],
+            scalar2=KEEP * KEEP + ALPHA * ALPHA,
+            op0=ALU.mult,
+            op1=ALU.add,
+        )
+        o_inv = inverse_root(nc, tail, o_sq[:, 0:1], "o_inv")
+        c_l = tail.tile([P, 1], F32)
+        nc.vector.tensor_scalar(
+            out=c_l[:], in0=o_inv[:], scalar1=ALPHA, scalar2=None, op0=ALU.mult
+        )
+        m_share = tail.tile([P, 1], F32)
+        nc.vector.tensor_scalar(
+            out=m_share[:],
+            in0=m_inv[:],
+            scalar1=l_norm[:, 0:1],
+            scalar2=KEEP,
+            op0=ALU.mult,
+            op1=ALU.mult,
+        )
+        c_m = tail.tile([P, 1], F32)
+        nc.vector.tensor_mul(out=c_m[:], in0=o_inv[:], in1=m_share[:])
+
+        per_store = STORE // K_PASS
+        for s in range(V // STORE):
+            cols = slice(s * STORE, (s + 1) * STORE)
+            scaled_logits = tail.tile([P, STORE], F32, tag="scaled_logits", bufs=2)
+            nc.scalar.activation(
+                out=scaled_logits[:], in_=logits_sb[:, cols], func=ACT.Copy, scale=c_l[:, 0:1]
+            )
+            result = tail.tile([P, STORE], F32, tag="result", bufs=3)
+            for j in range(per_store):
+                part = slice(j * K_PASS, (j + 1) * K_PASS)
+                bank = minted_bank(s * per_store + j)
+                nc.vector.scalar_tensor_tensor(
+                    out=result[:, part],
+                    in0=bank[:],
+                    scalar=c_m[:, 0:1],
+                    in1=scaled_logits[:, part],
+                    op0=ALU.mult,
+                    op1=ALU.add,
+                )
+            nc.sync.dma_start(out=out[:, cols], in_=result[:])

@@ -23,30 +23,14 @@ KEEP = 1.0 - ALPHA
 
 FLOPS = 2 * 2 * P * V * R
 
-PIECE = 4096
+PIECE = 2048
 PIECES = V // PIECE
+HALF = PIECE // 2
 STATS = 512
-L_CHUNK = 8
-STORE = 2048
-SCALAR_COLS = 224
-
-
-def inverse_root(nc, pool, x, name):
-    root = pool.tile([P, 1], F32, name=name + "_root")
-    nc.scalar.activation(out=root[:], in_=x, func=ACT.Sqrt)
-    rough = pool.tile([P, 1], F32, name=name + "_rough")
-    nc.vector.reciprocal(out=rough[:], in_=root[:])
-    unit = pool.tile([P, 1], F32, name=name + "_unit")
-    nc.vector.tensor_scalar(
-        out=unit[:], in0=rough[:], scalar1=x, scalar2=rough[:, 0:1], op0=ALU.mult, op1=ALU.mult
-    )
-    step = pool.tile([P, 1], F32, name=name + "_step")
-    nc.vector.tensor_scalar(
-        out=step[:], in0=unit[:], scalar1=-0.5, scalar2=1.5, op0=ALU.mult, op1=ALU.add
-    )
-    better = pool.tile([P, 1], F32, name=name)
-    nc.vector.tensor_mul(out=better[:], in0=rough[:], in1=step[:])
-    return better
+SHORT = 256
+L_CHUNK = 4
+STORE = 1024
+SCALAR_COLS = 192
 
 
 def tile_lowrankredistributor_k_kernel(tc, logits, W, out):
@@ -69,6 +53,11 @@ def tile_lowrankredistributor_k_kernel(tc, logits, W, out):
         wt_codes = keep.tile([P, GROUPS, K_PASS], U32, align_bytes=64)
         wt_scales = keep.tile([P, GROUPS, K_PASS], U8, align_bytes=64)
         l_norm = keep.tile([P, 1], F32)
+        l_inv = keep.tile([P, 1], F32)
+        h_bf = keep.tile([P, PACK, P], BF16)
+        h_by_r = keep.tile([P, P, PACK], BF16, align_bytes=64)
+        h_codes = keep.tile([P, P], U32, align_bytes=64)
+        h_scales = keep.tile([P, P], U8, align_bytes=64)
         h_acc = psum.tile([P, R], F32, tag="h_acc")
 
         for i in range(PIECES):
@@ -79,11 +68,70 @@ def tile_lowrankredistributor_k_kernel(tc, logits, W, out):
             early = first.enter_context(tc.tile_pool(name="early", bufs=1))
             stream = first.enter_context(tc.tile_pool(name="stream", bufs=3))
 
-            stats = early.tile([P, V // STATS, 6], F32)
-            for i in range(V // STATS):
-                nc.vector.bn_stats(
-                    out=stats[:, i, :], in_=logits_sb[:, i * STATS : (i + 1) * STATS]
-                )
+            stats = early.tile([P, PIECES * HALF // STATS, 6], F32)
+            sq_parts = early.tile([P, PIECES * HALF // SHORT], F32)
+            for i in range(PIECES):
+                for j in range(HALF // STATS):
+                    c0 = i * PIECE + j * STATS
+                    nc.vector.bn_stats(
+                        out=stats[:, i * (HALF // STATS) + j, :], in_=logits_sb[:, c0 : c0 + STATS]
+                    )
+                squares = stream.tile([P, HALF], BF16, tag="by_r", align_bytes=64)
+                for j in range(HALF // SHORT):
+                    c0 = i * PIECE + HALF + j * SHORT
+                    n = i * (HALF // SHORT) + j
+                    nc.scalar.activation(
+                        out=squares[:, j * SHORT : (j + 1) * SHORT],
+                        in_=logits_sb[:, c0 : c0 + SHORT],
+                        func=ACT.Square,
+                        accum_out=sq_parts[:, n : n + 1],
+                    )
+
+            mean_var = early.tile([P, 2], F32)
+            nc.vector.bn_aggr(out=mean_var[:], in_=stats[:].rearrange("p c s -> p (c s)"))
+            mean_sq = early.tile([P, 1], F32)
+            nc.vector.scalar_tensor_tensor(
+                out=mean_sq[:],
+                in0=mean_var[:, 0:1],
+                scalar=mean_var[:, 0:1],
+                in1=mean_var[:, 1:2],
+                op0=ALU.mult,
+                op1=ALU.add,
+            )
+            row_s = early.tile([P, 1], F32)
+            nc.vector.tensor_reduce(out=row_s[:], in_=sq_parts[:], axis=AXIS.X, op=ALU.add)
+            row = early.tile([P, 1], F32)
+            nc.vector.scalar_tensor_tensor(
+                out=row[:],
+                in0=mean_sq[:],
+                scalar=float(PIECES * HALF),
+                in1=row_s[:],
+                op0=ALU.mult,
+                op1=ALU.add,
+            )
+            l_sq_all = psum.tile([P, 1], F32, tag="small")
+            nc.tensor.matmul(out=l_sq_all[:], lhsT=ones[:], rhs=row[:], start=True, stop=True)
+            l_sq = early.tile([P, 1], F32)
+            nc.vector.tensor_copy(out=l_sq[:], in_=l_sq_all[:])
+            root = early.tile([P, 1], F32)
+            nc.scalar.activation(out=root[:], in_=l_sq[:], func=ACT.Sqrt)
+            rough = early.tile([P, 1], F32)
+            nc.vector.reciprocal(out=rough[:], in_=root[:])
+            unit = early.tile([P, 1], F32)
+            nc.vector.tensor_scalar(
+                out=unit[:],
+                in0=rough[:],
+                scalar1=l_sq[:, 0:1],
+                scalar2=rough[:, 0:1],
+                op0=ALU.mult,
+                op1=ALU.mult,
+            )
+            step_by = early.tile([P, 1], F32)
+            nc.vector.tensor_scalar(
+                out=step_by[:], in0=unit[:], scalar1=-0.5, scalar2=1.5, op0=ALU.mult, op1=ALU.add
+            )
+            nc.vector.tensor_mul(out=l_inv[:], in0=rough[:], in1=step_by[:])
+            nc.vector.tensor_mul(out=l_norm[:], in0=l_sq[:], in1=l_inv[:])
 
             lt = early.tile([P, GROUPS, P, PACK], BF16, align_bytes=64)
             lt_words = (
@@ -93,44 +141,23 @@ def tile_lowrankredistributor_k_kernel(tc, logits, W, out):
                 .rearrange("p (g b u) -> p g b u", b=P, u=2)
             )
             logit_words = logits_sb[:].bitcast(F32)
-            for pair in range(GROUPS // 2):
-                bank = psum.tile([P, 2, 2, P], F32, tag="bank", bufs=6)
-                for g2 in range(2):
-                    for u in range(2):
-                        w0 = 256 * (2 * pair + g2) + P * u
-                        nc.tensor.transpose(
-                            out=bank[:, g2, u, :],
-                            in_=logit_words[:, w0 : w0 + P],
-                            identity=ident_f32[:],
-                        )
-                nc.scalar.copy(
-                    out=lt_words[:, 2 * pair : 2 * pair + 2, :, :],
-                    in_=bank[:].rearrange("p g u b -> p g b u"),
-                )
-
-            mean_var = early.tile([P, 2], F32)
-            nc.vector.bn_aggr(out=mean_var[:], in_=stats[:].rearrange("p c s -> p (c s)"))
-            sq = early.tile([P, 1], F32)
-            nc.vector.scalar_tensor_tensor(
-                out=sq[:],
-                in0=mean_var[:, 0:1],
-                scalar=mean_var[:, 0:1],
-                in1=mean_var[:, 1:2],
-                op0=ALU.mult,
-                op1=ALU.add,
-            )
-            sq_all = psum.tile([P, 1], F32, tag="small")
-            nc.tensor.matmul(out=sq_all[:], lhsT=ones[:], rhs=sq[:], start=True, stop=True)
-            l_sq = early.tile([P, 1], F32)
-            nc.vector.tensor_scalar(
-                out=l_sq[:], in0=sq_all[:], scalar1=float(V), scalar2=None, op0=ALU.mult
-            )
-            l_inv = inverse_root(nc, keep, l_sq[:, 0:1], "l_inv")
-            nc.vector.tensor_mul(out=l_norm[:], in0=l_sq[:], in1=l_inv[:])
-
             l_codes = early.tile([P, GROUPS, P], U32, align_bytes=64)
             l_scales = early.tile([P, GROUPS, P], U8, align_bytes=64)
             for c in range(GROUPS // L_CHUNK):
+                for pair in range(c * L_CHUNK // 2, (c + 1) * L_CHUNK // 2):
+                    bank = psum.tile([P, 2, 2, P], F32, tag="bank", bufs=6)
+                    for g2 in range(2):
+                        for u in range(2):
+                            w0 = 256 * (2 * pair + g2) + P * u
+                            nc.tensor.transpose(
+                                out=bank[:, g2, u, :],
+                                in_=logit_words[:, w0 : w0 + P],
+                                identity=ident_f32[:],
+                            )
+                    nc.scalar.copy(
+                        out=lt_words[:, 2 * pair : 2 * pair + 2, :, :],
+                        in_=bank[:].rearrange("p g u b -> p g b u"),
+                    )
                 gs = slice(c * L_CHUNK, (c + 1) * L_CHUNK)
                 chunk = lt[:, gs].rearrange("p g b t -> p (g b t)")
                 nc.vector.tensor_scalar(
@@ -143,36 +170,63 @@ def tile_lowrankredistributor_k_kernel(tc, logits, W, out):
                 )
 
             w_rows = W.rearrange("(c p e) r -> p c (e r)", p=P, e=2)
-            for g in range(GROUPS):
-                raw = stream.tile([P, PACK, R], BF16, tag="raw", bufs=5)
+            raw = {}
+            by_v = {}
+            by_r = {}
+            banks = {}
+            w0_codes = {}
+            w0_scales = {}
+
+            def load(g):
+                raw[g] = stream.tile([P, PACK, R], BF16, tag="raw", bufs=5, name="raw")
                 nc.sync.dma_start(
-                    out=raw[:].rearrange("p (u e) r -> p u (e r)", e=2),
+                    out=raw[g][:].rearrange("p (u e) r -> p u (e r)", e=2),
                     in_=w_rows[:, 2 * g : 2 * g + 2, :],
                 )
 
-                by_v = stream.tile([P, R, PACK], BF16, tag="by_v", align_bytes=64)
+            def regroup(g):
+                by_v[g] = stream.tile([P, R, PACK], BF16, tag="by_v", align_bytes=64, name="by_v")
                 nc.scalar.copy(
-                    out=by_v[:, :SCALAR_COLS, :].rearrange("p (c i) t -> p c t i", i=4),
-                    in_=raw[:, :, :SCALAR_COLS].rearrange("p t (c i) -> p c t i", i=4),
+                    out=by_v[g][:, :SCALAR_COLS, :].rearrange("p (c i) t -> p c t i", i=4),
+                    in_=raw[g][:, :, :SCALAR_COLS].rearrange("p t (c i) -> p c t i", i=4),
                 )
                 nc.vector.tensor_copy(
-                    out=by_v[:, SCALAR_COLS:, :].rearrange("p (c i) t -> p c t i", i=4),
-                    in_=raw[:, :, SCALAR_COLS:].rearrange("p t (c i) -> p c t i", i=4),
+                    out=by_v[g][:, SCALAR_COLS:, :].rearrange("p (c i) t -> p c t i", i=4),
+                    in_=raw[g][:, :, SCALAR_COLS:].rearrange("p t (c i) -> p c t i", i=4),
                 )
 
+            def quantise_by_v(g):
+                w0_codes[g] = stream.tile(
+                    [P, R], U32, tag="w0_codes", bufs=4, align_bytes=64, name="w0_codes"
+                )
+                w0_scales[g] = stream.tile(
+                    [P, R], U8, tag="w0_scales", bufs=4, align_bytes=64, name="w0_scales"
+                )
+                nc.vector.quantize_mx(
+                    out=w0_codes[g][:].bitcast(FP8X4),
+                    scales=w0_scales[g][:],
+                    in_=by_v[g][:].rearrange("p r t -> p (r t)"),
+                )
+
+            def first_matmul(g):
+                nc.tensor.matmul_mx(
+                    out=h_acc[:],
+                    lhsT=l_codes[:, g, :].bitcast(FP8X4),
+                    lhsT_scale=l_scales[:, g, :],
+                    rhs=w0_codes[g][:].bitcast(FP8X4),
+                    rhs_scale=w0_scales[g][:],
+                    start=(g == 0),
+                    stop=(g == GROUPS - 1),
+                )
+
+            def transpose(g):
                 raw_words = (
-                    raw[:]
+                    raw[g][:]
                     .rearrange("p t r -> p (t r)")
                     .bitcast(F32)
                     .rearrange("p (t w) -> p t w", t=PACK)
                 )
-                by_r = stream.tile([P, K_PASS, PACK], BF16, tag="by_r", align_bytes=64)
-                by_r_words = (
-                    by_r[:]
-                    .rearrange("q n t -> q (n t)")
-                    .bitcast(F32)
-                    .rearrange("q (a p e u) -> q a p e u", a=2, e=2, u=2)
-                )
+                banks[g] = []
                 for a in range(2):
                     bank = psum.tile([P, 2, 2, P], F32, tag="bank", bufs=6)
                     for e in range(2):
@@ -182,51 +236,64 @@ def tile_lowrankredistributor_k_kernel(tc, logits, W, out):
                                 in_=raw_words[:, 2 * a + e, P * u : P * u + P],
                                 identity=ident_f32[:],
                             )
+                    banks[g].append(bank)
+
+            def empty_banks(g):
+                by_r[g] = stream.tile(
+                    [P, K_PASS, PACK], BF16, tag="by_r", align_bytes=64, name="by_r"
+                )
+                by_r_words = (
+                    by_r[g][:]
+                    .rearrange("q n t -> q (n t)")
+                    .bitcast(F32)
+                    .rearrange("q (a p e u) -> q a p e u", a=2, e=2, u=2)
+                )
+                for a in range(2):
                     nc.scalar.copy(
-                        out=by_r_words[:, a], in_=bank[:].rearrange("q e u p -> q p e u")
+                        out=by_r_words[:, a], in_=banks[g][a][:].rearrange("q e u p -> q p e u")
                     )
 
-                w0_codes = stream.tile([P, R], U32, tag="w0_codes", bufs=4, align_bytes=64)
-                w0_scales = stream.tile([P, R], U8, tag="w0_scales", bufs=4, align_bytes=64)
-                nc.vector.quantize_mx(
-                    out=w0_codes[:].bitcast(FP8X4),
-                    scales=w0_scales[:],
-                    in_=by_v[:].rearrange("p r t -> p (r t)"),
-                )
+            def quantise_by_r(g):
                 nc.vector.quantize_mx(
                     out=wt_codes[:, g, :].bitcast(FP8X4),
                     scales=wt_scales[:, g, :],
-                    in_=by_r[:].rearrange("q n t -> q (n t)"),
-                )
-                nc.tensor.matmul_mx(
-                    out=h_acc[:],
-                    lhsT=l_codes[:, g, :].bitcast(FP8X4),
-                    lhsT_scale=l_scales[:, g, :],
-                    rhs=w0_codes[:].bitcast(FP8X4),
-                    rhs_scale=w0_scales[:],
-                    start=(g == 0),
-                    stop=(g == GROUPS - 1),
+                    in_=by_r[g][:].rearrange("q n t -> q (n t)"),
                 )
 
-        tail = ctx.enter_context(tc.tile_pool(name="tail", bufs=1))
+            def step(s):
+                if s < GROUPS:
+                    load(s)
+                    regroup(s)
+                if 0 <= s - 1 < GROUPS:
+                    transpose(s - 1)
+                    quantise_by_v(s - 1)
+                if 0 <= s - 2 < GROUPS:
+                    first_matmul(s - 2)
+                if 0 <= s - 3 < GROUPS:
+                    empty_banks(s - 3)
+                if 0 <= s - 4 < GROUPS:
+                    quantise_by_r(s - 4)
 
-        h_bf = tail.tile([P, PACK, P], BF16)
-        nc.vector.tensor_copy(
-            out=h_bf[:].rearrange("b (u e) q -> b u e q", e=2),
-            in_=h_acc[:].rearrange("b (u q e) -> b u e q", u=2, e=2),
-        )
-        h_t = psum.tile([P, PACK, P], BF16, tag="small")
-        for t in range(PACK):
-            nc.tensor.transpose(out=h_t[:, t, :], in_=h_bf[:, t, :], identity=ident_bf[:])
-        h_by_r = tail.tile([P, P, PACK], BF16, align_bytes=64)
-        nc.vector.tensor_copy(out=h_by_r[:], in_=h_t[:].rearrange("q t b -> q b t"))
-        h_codes = tail.tile([P, P], U32, align_bytes=64)
-        h_scales = tail.tile([P, P], U8, align_bytes=64)
-        nc.vector.quantize_mx(
-            out=h_codes[:].bitcast(FP8X4),
-            scales=h_scales[:],
-            in_=h_by_r[:].rearrange("q b t -> q (b t)"),
-        )
+            for s in range(GROUPS + 2):
+                step(s)
+
+            nc.vector.tensor_copy(
+                out=h_bf[:].rearrange("b (u e) q -> b u e q", e=2),
+                in_=h_acc[:].rearrange("b (u q e) -> b u e q", u=2, e=2),
+            )
+            h_t = psum.tile([P, PACK, P], BF16, tag="small")
+            for t in range(PACK):
+                nc.tensor.transpose(out=h_t[:, t, :], in_=h_bf[:, t, :], identity=ident_bf[:])
+            step(GROUPS + 2)
+            nc.vector.tensor_copy(out=h_by_r[:], in_=h_t[:].rearrange("q t b -> q b t"))
+            step(GROUPS + 3)
+            nc.vector.quantize_mx(
+                out=h_codes[:].bitcast(FP8X4),
+                scales=h_scales[:],
+                in_=h_by_r[:].rearrange("q b t -> q (b t)"),
+            )
+
+        tail = ctx.enter_context(tc.tile_pool(name="tail", bufs=1, reuse_waits="tile"))
 
         def minted_bank(g):
             bank = psum.tile([P, K_PASS], F32, tag="bank", bufs=6)
@@ -266,52 +333,52 @@ def tile_lowrankredistributor_k_kernel(tc, logits, W, out):
         nc.vector.tensor_reduce(out=sums[:, 1:2], in_=ml_parts[:], axis=AXIS.X, op=ALU.add)
         sums_all = psum.tile([P, 2], F32, tag="small")
         nc.tensor.matmul(out=sums_all[:], lhsT=ones[:], rhs=sums[:], start=True, stop=True)
-        totals = tail.tile([P, 2], F32)
-        nc.vector.tensor_copy(out=totals[:], in_=sums_all[:])
-        m_inv = inverse_root(nc, tail, totals[:, 0:1], "m_inv")
+        m_norm = tail.tile([P, 1], F32)
+        nc.scalar.activation(out=m_norm[:], in_=sums_all[:, 0:1], func=ACT.Sqrt)
+        m_inv = tail.tile([P, 1], F32)
+        nc.vector.reciprocal(out=m_inv[:], in_=m_norm[:])
         both_inv = tail.tile([P, 1], F32)
         nc.vector.tensor_scalar(
             out=both_inv[:],
             in0=m_inv[:],
             scalar1=l_inv[:, 0:1],
-            scalar2=2.0 * KEEP * ALPHA,
+            scalar2=2.0 * KEEP / ALPHA,
             op0=ALU.mult,
             op1=ALU.mult,
         )
         o_sq = tail.tile([P, 1], F32)
         nc.vector.tensor_scalar(
             out=o_sq[:],
-            in0=totals[:, 1:2],
+            in0=sums_all[:, 1:2],
             scalar1=both_inv[:, 0:1],
-            scalar2=KEEP * KEEP + ALPHA * ALPHA,
+            scalar2=(KEEP * KEEP + ALPHA * ALPHA) / (ALPHA * ALPHA),
             op0=ALU.mult,
             op1=ALU.add,
         )
-        o_inv = inverse_root(nc, tail, o_sq[:, 0:1], "o_inv")
-        c_l = tail.tile([P, 1], F32)
+        o_norm = tail.tile([P, 1], F32)
+        nc.scalar.activation(out=o_norm[:], in_=o_sq[:], func=ACT.Sqrt)
+        ratio = tail.tile([P, 1], F32)
         nc.vector.tensor_scalar(
-            out=c_l[:], in0=o_inv[:], scalar1=ALPHA, scalar2=None, op0=ALU.mult
-        )
-        m_share = tail.tile([P, 1], F32)
-        nc.vector.tensor_scalar(
-            out=m_share[:],
+            out=ratio[:],
             in0=m_inv[:],
             scalar1=l_norm[:, 0:1],
-            scalar2=KEEP,
+            scalar2=KEEP / ALPHA,
             op0=ALU.mult,
             op1=ALU.mult,
         )
+        c_l = tail.tile([P, 1], F32)
+        nc.vector.reciprocal(out=c_l[:], in_=o_norm[:])
         c_m = tail.tile([P, 1], F32)
-        nc.vector.tensor_mul(out=c_m[:], in0=o_inv[:], in1=m_share[:])
+        nc.vector.tensor_mul(out=c_m[:], in0=c_l[:], in1=ratio[:])
 
         per_store = STORE // K_PASS
         for s in range(V // STORE):
             cols = slice(s * STORE, (s + 1) * STORE)
-            scaled_logits = tail.tile([P, STORE], F32, tag="scaled_logits", bufs=2)
+            scaled_logits = tail.tile([P, STORE], F32, tag="scaled_logits", bufs=3)
             nc.scalar.activation(
                 out=scaled_logits[:], in_=logits_sb[:, cols], func=ACT.Copy, scale=c_l[:, 0:1]
             )
-            result = tail.tile([P, STORE], F32, tag="result", bufs=3)
+            result = tail.tile([P, STORE], F32, tag="result", bufs=4)
             for j in range(per_store):
                 part = slice(j * K_PASS, (j + 1) * K_PASS)
                 bank = minted_bank(s * per_store + j)

@@ -31,6 +31,7 @@ SHORT = 256
 L_CHUNK = 4
 STORE = 1024
 SCALAR_COLS = 192
+MX_RUN = 2
 
 
 def tile_lowrankredistributor_k_kernel(tc, logits, W, out):
@@ -197,10 +198,10 @@ def tile_lowrankredistributor_k_kernel(tc, logits, W, out):
 
             def quantise_by_v(g):
                 w0_codes[g] = stream.tile(
-                    [P, R], U32, tag="w0_codes", bufs=4, align_bytes=64, name="w0_codes"
+                    [P, R], U32, tag="w0_codes", bufs=MX_RUN + 3, align_bytes=64, name="w0_codes"
                 )
                 w0_scales[g] = stream.tile(
-                    [P, R], U8, tag="w0_scales", bufs=4, align_bytes=64, name="w0_scales"
+                    [P, R], U8, tag="w0_scales", bufs=MX_RUN + 3, align_bytes=64, name="w0_scales"
                 )
                 nc.vector.quantize_mx(
                     out=w0_codes[g][:].bitcast(FP8X4),
@@ -267,31 +268,33 @@ def tile_lowrankredistributor_k_kernel(tc, logits, W, out):
                 if 0 <= s - 1 < GROUPS:
                     transpose(s - 1)
                     quantise_by_v(s - 1)
-                if 0 <= s - 2 < GROUPS:
-                    first_matmul(s - 2)
+                if s % MX_RUN == MX_RUN - 1:
+                    for g in range(max(s - 1 - MX_RUN, 0), min(s - 1, GROUPS)):
+                        first_matmul(g)
                 if 0 <= s - 3 < GROUPS:
                     empty_banks(s - 3)
                 if 0 <= s - 4 < GROUPS:
                     quantise_by_r(s - 4)
 
-            for s in range(GROUPS + 2):
-                step(s)
+            with tc.manual_schedule():
+                for s in range(GROUPS + 2):
+                    step(s)
 
-            nc.vector.tensor_copy(
-                out=h_bf[:].rearrange("b (u e) q -> b u e q", e=2),
-                in_=h_acc[:].rearrange("b (u q e) -> b u e q", u=2, e=2),
-            )
-            h_t = psum.tile([P, PACK, P], BF16, tag="small")
-            for t in range(PACK):
-                nc.tensor.transpose(out=h_t[:, t, :], in_=h_bf[:, t, :], identity=ident_bf[:])
-            step(GROUPS + 2)
-            nc.vector.tensor_copy(out=h_by_r[:], in_=h_t[:].rearrange("q t b -> q b t"))
-            step(GROUPS + 3)
-            nc.vector.quantize_mx(
-                out=h_codes[:].bitcast(FP8X4),
-                scales=h_scales[:],
-                in_=h_by_r[:].rearrange("q b t -> q (b t)"),
-            )
+                nc.vector.tensor_copy(
+                    out=h_bf[:].rearrange("b (u e) q -> b u e q", e=2),
+                    in_=h_acc[:].rearrange("b (u q e) -> b u e q", u=2, e=2),
+                )
+                h_t = psum.tile([P, PACK, P], BF16, tag="small")
+                for t in range(PACK):
+                    nc.tensor.transpose(out=h_t[:, t, :], in_=h_bf[:, t, :], identity=ident_bf[:])
+                step(GROUPS + 2)
+                nc.vector.tensor_copy(out=h_by_r[:], in_=h_t[:].rearrange("q t b -> q b t"))
+                step(GROUPS + 3)
+                nc.vector.quantize_mx(
+                    out=h_codes[:].bitcast(FP8X4),
+                    scales=h_scales[:],
+                    in_=h_by_r[:].rearrange("q b t -> q (b t)"),
+                )
 
         tail = ctx.enter_context(tc.tile_pool(name="tail", bufs=1, reuse_waits="tile"))
 

@@ -31,7 +31,7 @@ SHORT = 256
 L_CHUNK = 4
 STORE = 1024
 SCALAR_COLS = 192
-MX_RUN = 2
+MX_RUN = 4
 
 
 def tile_lowrankredistributor_k_kernel(tc, logits, W, out):
@@ -268,7 +268,7 @@ def tile_lowrankredistributor_k_kernel(tc, logits, W, out):
                 if 0 <= s - 1 < GROUPS:
                     transpose(s - 1)
                     quantise_by_v(s - 1)
-                if s % MX_RUN == MX_RUN - 1:
+                if (GROUPS + 1 - s) % MX_RUN == 0:
                     for g in range(max(s - 1 - MX_RUN, 0), min(s - 1, GROUPS)):
                         first_matmul(g)
                 if 0 <= s - 3 < GROUPS:
@@ -340,6 +340,15 @@ def tile_lowrankredistributor_k_kernel(tc, logits, W, out):
         nc.scalar.activation(out=m_norm[:], in_=sums_all[:, 0:1], func=ACT.Sqrt)
         m_inv = tail.tile([P, 1], F32)
         nc.vector.reciprocal(out=m_inv[:], in_=m_norm[:])
+        ratio = tail.tile([P, 1], F32)
+        nc.vector.tensor_scalar(
+            out=ratio[:],
+            in0=m_inv[:],
+            scalar1=l_norm[:, 0:1],
+            scalar2=KEEP / ALPHA,
+            op0=ALU.mult,
+            op1=ALU.mult,
+        )
         both_inv = tail.tile([P, 1], F32)
         nc.vector.tensor_scalar(
             out=both_inv[:],
@@ -360,37 +369,34 @@ def tile_lowrankredistributor_k_kernel(tc, logits, W, out):
         )
         o_norm = tail.tile([P, 1], F32)
         nc.scalar.activation(out=o_norm[:], in_=o_sq[:], func=ACT.Sqrt)
-        ratio = tail.tile([P, 1], F32)
-        nc.vector.tensor_scalar(
-            out=ratio[:],
-            in0=m_inv[:],
-            scalar1=l_norm[:, 0:1],
-            scalar2=KEEP / ALPHA,
-            op0=ALU.mult,
-            op1=ALU.mult,
-        )
         c_l = tail.tile([P, 1], F32)
         nc.vector.reciprocal(out=c_l[:], in_=o_norm[:])
-        c_m = tail.tile([P, 1], F32)
-        nc.vector.tensor_mul(out=c_m[:], in0=c_l[:], in1=ratio[:])
 
         per_store = STORE // K_PASS
-        for s in range(V // STORE):
-            cols = slice(s * STORE, (s + 1) * STORE)
-            scaled_logits = tail.tile([P, STORE], F32, tag="scaled_logits", bufs=3)
-            nc.scalar.activation(
-                out=scaled_logits[:], in_=logits_sb[:, cols], func=ACT.Copy, scale=c_l[:, 0:1]
-            )
-            result = tail.tile([P, STORE], F32, tag="result", bufs=4)
+        for k in range(V // STORE):
+            result = tail.tile([P, STORE], F32, tag="result", bufs=6)
             for j in range(per_store):
-                part = slice(j * K_PASS, (j + 1) * K_PASS)
-                bank = minted_bank(s * per_store + j)
+                g = k * per_store + j
+                bank = minted_bank(g)
                 nc.vector.scalar_tensor_tensor(
-                    out=result[:, part],
+                    out=result[:, j * K_PASS : (j + 1) * K_PASS],
                     in0=bank[:],
-                    scalar=c_m[:, 0:1],
-                    in1=scaled_logits[:, part],
+                    scalar=ratio[:, 0:1],
+                    in1=logits_sb[:, g * K_PASS : (g + 1) * K_PASS],
                     op0=ALU.mult,
                     op1=ALU.add,
                 )
-            nc.sync.dma_start(out=out[:, cols], in_=result[:])
+            if k % 3 == 1:
+                nc.gpsimd.tensor_scalar(
+                    out=result[:],
+                    in0=result[:],
+                    scalar1=c_l[:, 0:1],
+                    scalar2=0.0,
+                    op0=ALU.mult,
+                    op1=ALU.add,
+                )
+            else:
+                nc.scalar.activation(
+                    out=result[:], in_=result[:], func=ACT.Copy, scale=c_l[:, 0:1]
+                )
+            nc.sync.dma_start(out=out[:, k * STORE : (k + 1) * STORE], in_=result[:])

@@ -60,6 +60,8 @@ def tile_lowrankredistributor_k_kernel(tc, logits, W, out):
         h_codes = keep.tile([P, P], U32, align_bytes=64)
         h_scales = keep.tile([P, P], U8, align_bytes=64)
         h_acc = psum.tile([P, R], F32, tag="h_acc")
+        h_sq = keep.tile([P, 1], F32)
+        h_squares = keep.tile([P, R], BF16)
 
         for i in range(PIECES):
             cols = slice(i * PIECE, (i + 1) * PIECE)
@@ -284,6 +286,9 @@ def tile_lowrankredistributor_k_kernel(tc, logits, W, out):
                     out=h_bf[:].rearrange("b (u e) q -> b u e q", e=2),
                     in_=h_acc[:].rearrange("b (u q e) -> b u e q", u=2, e=2),
                 )
+                nc.scalar.activation(
+                    out=h_squares[:], in_=h_acc[:], func=ACT.Square, accum_out=h_sq[:, 0:1]
+                )
                 h_t = psum.tile([P, PACK, P], BF16, tag="small")
                 for t in range(PACK):
                     nc.tensor.transpose(out=h_t[:, t, :], in_=h_bf[:, t, :], identity=ident_bf[:])
@@ -311,29 +316,44 @@ def tile_lowrankredistributor_k_kernel(tc, logits, W, out):
             )
             return bank
 
-        mm_parts = tail.tile([P, GROUPS], F32)
-        ml_parts = tail.tile([P, GROUPS], F32)
+        mm_parts = tail.tile([P, GROUPS // 2], F32)
+        m_stats = tail.tile([P, GROUPS // 2, 6], F32)
         for g in range(GROUPS):
-            cols = slice(g * K_PASS, (g + 1) * K_PASS)
             bank = minted_bank(g)
-            junk_s = tail.tile([P, K_PASS], BF16, tag="junk_s", bufs=4)
-            nc.scalar.activation(
-                out=junk_s[:], in_=bank[:], func=ACT.Square, accum_out=mm_parts[:, g : g + 1]
-            )
-            junk_v = tail.tile([P, K_PASS], F32, tag="junk_v", bufs=4)
-            nc.vector.scalar_tensor_tensor(
-                out=junk_v[:],
-                in0=bank[:],
-                scalar=1.0,
-                in1=logits_sb[:, cols],
-                op0=ALU.mult,
-                op1=ALU.mult,
-                accum_out=ml_parts[:, g : g + 1],
-            )
+            if g % 2 == 0:
+                junk_s = tail.tile([P, K_PASS], BF16, tag="junk_s", bufs=4)
+                nc.scalar.activation(
+                    out=junk_s[:],
+                    in_=bank[:],
+                    func=ACT.Square,
+                    accum_out=mm_parts[:, g // 2 : g // 2 + 1],
+                )
+            else:
+                nc.vector.bn_stats(out=m_stats[:, g // 2, :], in_=bank[:])
 
+        m_mean_var = tail.tile([P, 2], F32)
+        nc.vector.bn_aggr(out=m_mean_var[:], in_=m_stats[:].rearrange("p c s -> p (c s)"))
+        m_mean_sq = tail.tile([P, 1], F32)
+        nc.vector.scalar_tensor_tensor(
+            out=m_mean_sq[:],
+            in0=m_mean_var[:, 0:1],
+            scalar=m_mean_var[:, 0:1],
+            in1=m_mean_var[:, 1:2],
+            op0=ALU.mult,
+            op1=ALU.add,
+        )
+        mm_row = tail.tile([P, 1], F32)
+        nc.vector.tensor_reduce(out=mm_row[:], in_=mm_parts[:], axis=AXIS.X, op=ALU.add)
         sums = tail.tile([P, 2], F32)
-        nc.vector.tensor_reduce(out=sums[:, 0:1], in_=mm_parts[:], axis=AXIS.X, op=ALU.add)
-        nc.vector.tensor_reduce(out=sums[:, 1:2], in_=ml_parts[:], axis=AXIS.X, op=ALU.add)
+        nc.vector.scalar_tensor_tensor(
+            out=sums[:, 0:1],
+            in0=m_mean_sq[:],
+            scalar=float(V // 2),
+            in1=mm_row[:],
+            op0=ALU.mult,
+            op1=ALU.add,
+        )
+        nc.vector.tensor_copy(out=sums[:, 1:2], in_=h_sq[:])
         sums_all = psum.tile([P, 2], F32, tag="small")
         nc.tensor.matmul(out=sums_all[:], lhsT=ones[:], rhs=sums[:], start=True, stop=True)
         m_norm = tail.tile([P, 1], F32)
@@ -349,20 +369,13 @@ def tile_lowrankredistributor_k_kernel(tc, logits, W, out):
             op0=ALU.mult,
             op1=ALU.mult,
         )
-        both_inv = tail.tile([P, 1], F32)
-        nc.vector.tensor_scalar(
-            out=both_inv[:],
-            in0=m_inv[:],
-            scalar1=l_inv[:, 0:1],
-            scalar2=2.0 * KEEP / ALPHA,
-            op0=ALU.mult,
-            op1=ALU.mult,
-        )
+        cosine = tail.tile([P, 1], F32)
+        nc.vector.tensor_mul(out=cosine[:], in0=sums_all[:, 1:2], in1=m_inv[:])
         o_sq = tail.tile([P, 1], F32)
         nc.vector.tensor_scalar(
             out=o_sq[:],
-            in0=sums_all[:, 1:2],
-            scalar1=both_inv[:, 0:1],
+            in0=cosine[:],
+            scalar1=2.0 * KEEP / ALPHA,
             scalar2=(KEEP * KEEP + ALPHA * ALPHA) / (ALPHA * ALPHA),
             op0=ALU.mult,
             op1=ALU.add,

@@ -25,12 +25,14 @@ FLOPS = 2 * 2 * P * V * R
 
 PIECE = 2048
 PIECES = V // PIECE
-HALF = PIECE // 2
 STATS = 512
-SHORT = 256
+GRAM = (PIECE - STATS) // P
+W_EVERY = 2
+LEAD = (PIECES + W_EVERY - 1) // W_EVERY
 L_CHUNK = 4
 STORE = 1024
-SCALAR_COLS = 192
+SCALAR_COLS = 208
+SCALAR_COLS_L = 320
 MX_RUN = 4
 
 
@@ -63,79 +65,12 @@ def tile_lowrankredistributor_k_kernel(tc, logits, W, out):
         h_sq = keep.tile([P, 1], F32)
         h_squares = keep.tile([P, R], BF16)
 
-        for i in range(PIECES):
-            cols = slice(i * PIECE, (i + 1) * PIECE)
-            nc.sync.dma_start(out=logits_sb[:, cols], in_=logits[:, cols])
-
         with ExitStack() as first:
             early = first.enter_context(tc.tile_pool(name="early", bufs=1))
             stream = first.enter_context(tc.tile_pool(name="stream", bufs=3))
 
-            stats = early.tile([P, PIECES * HALF // STATS, 6], F32)
-            sq_parts = early.tile([P, PIECES * HALF // SHORT], F32)
-            for i in range(PIECES):
-                for j in range(HALF // STATS):
-                    c0 = i * PIECE + j * STATS
-                    nc.vector.bn_stats(
-                        out=stats[:, i * (HALF // STATS) + j, :], in_=logits_sb[:, c0 : c0 + STATS]
-                    )
-                squares = stream.tile([P, HALF], BF16, tag="by_r", align_bytes=64)
-                for j in range(HALF // SHORT):
-                    c0 = i * PIECE + HALF + j * SHORT
-                    n = i * (HALF // SHORT) + j
-                    nc.scalar.activation(
-                        out=squares[:, j * SHORT : (j + 1) * SHORT],
-                        in_=logits_sb[:, c0 : c0 + SHORT],
-                        func=ACT.Square,
-                        accum_out=sq_parts[:, n : n + 1],
-                    )
-
-            mean_var = early.tile([P, 2], F32)
-            nc.vector.bn_aggr(out=mean_var[:], in_=stats[:].rearrange("p c s -> p (c s)"))
-            mean_sq = early.tile([P, 1], F32)
-            nc.vector.scalar_tensor_tensor(
-                out=mean_sq[:],
-                in0=mean_var[:, 0:1],
-                scalar=mean_var[:, 0:1],
-                in1=mean_var[:, 1:2],
-                op0=ALU.mult,
-                op1=ALU.add,
-            )
-            row_s = early.tile([P, 1], F32)
-            nc.vector.tensor_reduce(out=row_s[:], in_=sq_parts[:], axis=AXIS.X, op=ALU.add)
-            row = early.tile([P, 1], F32)
-            nc.vector.scalar_tensor_tensor(
-                out=row[:],
-                in0=mean_sq[:],
-                scalar=float(PIECES * HALF),
-                in1=row_s[:],
-                op0=ALU.mult,
-                op1=ALU.add,
-            )
-            l_sq_all = psum.tile([P, 1], F32, tag="small")
-            nc.tensor.matmul(out=l_sq_all[:], lhsT=ones[:], rhs=row[:], start=True, stop=True)
-            l_sq = early.tile([P, 1], F32)
-            nc.vector.tensor_copy(out=l_sq[:], in_=l_sq_all[:])
-            root = early.tile([P, 1], F32)
-            nc.scalar.activation(out=root[:], in_=l_sq[:], func=ACT.Sqrt)
-            rough = early.tile([P, 1], F32)
-            nc.vector.reciprocal(out=rough[:], in_=root[:])
-            unit = early.tile([P, 1], F32)
-            nc.vector.tensor_scalar(
-                out=unit[:],
-                in0=rough[:],
-                scalar1=l_sq[:, 0:1],
-                scalar2=rough[:, 0:1],
-                op0=ALU.mult,
-                op1=ALU.mult,
-            )
-            step_by = early.tile([P, 1], F32)
-            nc.vector.tensor_scalar(
-                out=step_by[:], in0=unit[:], scalar1=-0.5, scalar2=1.5, op0=ALU.mult, op1=ALU.add
-            )
-            nc.vector.tensor_mul(out=l_inv[:], in0=rough[:], in1=step_by[:])
-            nc.vector.tensor_mul(out=l_norm[:], in0=l_sq[:], in1=l_inv[:])
-
+            stats = early.tile([P, PIECES, 6], F32)
+            squares = psum.tile([P, P], F32, tag="small")
             lt = early.tile([P, GROUPS, P, PACK], BF16, align_bytes=64)
             lt_words = (
                 lt[:]
@@ -146,30 +81,66 @@ def tile_lowrankredistributor_k_kernel(tc, logits, W, out):
             logit_words = logits_sb[:].bitcast(F32)
             l_codes = early.tile([P, GROUPS, P], U32, align_bytes=64)
             l_scales = early.tile([P, GROUPS, P], U8, align_bytes=64)
-            for c in range(GROUPS // L_CHUNK):
-                for pair in range(c * L_CHUNK // 2, (c + 1) * L_CHUNK // 2):
+            l_banks = {}
+
+            def load_logits(i):
+                cols = slice(i * PIECE, (i + 1) * PIECE)
+                nc.sync.dma_start(out=logits_sb[:, cols], in_=logits[:, cols])
+
+            def square_logits(i):
+                for j in range(GRAM):
+                    block = logits_sb[:, i * PIECE + j * P : i * PIECE + (j + 1) * P]
+                    nc.tensor.matmul(
+                        out=squares[:],
+                        lhsT=block,
+                        rhs=block,
+                        start=(i == 0 and j == 0),
+                        stop=(i == PIECES - 1 and j == GRAM - 1),
+                    )
+                nc.vector.bn_stats(
+                    out=stats[:, i, :], in_=logits_sb[:, (i + 1) * PIECE - STATS : (i + 1) * PIECE]
+                )
+
+            def transpose_logits(i):
+                l_banks[i] = []
+                for pair in range(2):
                     bank = psum.tile([P, 2, 2, P], F32, tag="bank", bufs=6)
                     for g2 in range(2):
                         for u in range(2):
-                            w0 = 256 * (2 * pair + g2) + P * u
+                            w0 = i * PIECE // 2 + 256 * (2 * pair + g2) + P * u
                             nc.tensor.transpose(
                                 out=bank[:, g2, u, :],
                                 in_=logit_words[:, w0 : w0 + P],
                                 identity=ident_f32[:],
                             )
+                    l_banks[i].append(bank)
+
+            def empty_logits(i):
+                for pair in range(2):
+                    g0 = i * PIECE // K_PASS + 2 * pair
                     nc.scalar.copy(
-                        out=lt_words[:, 2 * pair : 2 * pair + 2, :, :],
-                        in_=bank[:].rearrange("p g u b -> p g b u"),
+                        out=lt_words[:, g0 : g0 + 2, :, :],
+                        in_=l_banks[i][pair][:].rearrange("p g u b -> p g b u"),
                     )
-                gs = slice(c * L_CHUNK, (c + 1) * L_CHUNK)
-                chunk = lt[:, gs].rearrange("p g b t -> p (g b t)")
+
+            def lt_chunk(c):
+                return lt[:, c * L_CHUNK : (c + 1) * L_CHUNK].rearrange("p g b t -> p (g b t)")
+
+            def scale_logits(c):
                 nc.vector.tensor_scalar(
-                    out=chunk, in0=chunk, scalar1=l_inv[:, 0:1], scalar2=None, op0=ALU.mult
+                    out=lt_chunk(c),
+                    in0=lt_chunk(c),
+                    scalar1=l_inv[:, 0:1],
+                    scalar2=None,
+                    op0=ALU.mult,
                 )
+
+            def quantise_logits(c):
+                gs = slice(c * L_CHUNK, (c + 1) * L_CHUNK)
                 nc.vector.quantize_mx(
                     out=l_codes[:, gs, :].rearrange("p g b -> p (g b)").bitcast(FP8X4),
                     scales=l_scales[:, gs, :].rearrange("p g b -> p (g b)"),
-                    in_=chunk,
+                    in_=lt_chunk(c),
                 )
 
             w_rows = W.rearrange("(c p e) r -> p c (e r)", p=P, e=2)
@@ -181,29 +152,30 @@ def tile_lowrankredistributor_k_kernel(tc, logits, W, out):
             w0_scales = {}
 
             def load(g):
-                raw[g] = stream.tile([P, PACK, R], BF16, tag="raw", bufs=5, name="raw")
+                raw[g] = stream.tile([P, PACK, R], BF16, tag="raw", bufs=6, name="raw")
                 nc.sync.dma_start(
                     out=raw[g][:].rearrange("p (u e) r -> p u (e r)", e=2),
                     in_=w_rows[:, 2 * g : 2 * g + 2, :],
                 )
 
-            def regroup(g):
+            def regroup(g, scalar_cols):
                 by_v[g] = stream.tile([P, R, PACK], BF16, tag="by_v", align_bytes=64, name="by_v")
-                nc.scalar.copy(
-                    out=by_v[g][:, :SCALAR_COLS, :].rearrange("p (c i) t -> p c t i", i=4),
-                    in_=raw[g][:, :, :SCALAR_COLS].rearrange("p t (c i) -> p c t i", i=4),
-                )
+                if scalar_cols > 0:
+                    nc.scalar.copy(
+                        out=by_v[g][:, :scalar_cols, :].rearrange("p (c i) t -> p c t i", i=4),
+                        in_=raw[g][:, :, :scalar_cols].rearrange("p t (c i) -> p c t i", i=4),
+                    )
                 nc.vector.tensor_copy(
-                    out=by_v[g][:, SCALAR_COLS:, :].rearrange("p (c i) t -> p c t i", i=4),
-                    in_=raw[g][:, :, SCALAR_COLS:].rearrange("p t (c i) -> p c t i", i=4),
+                    out=by_v[g][:, scalar_cols:, :].rearrange("p (c i) t -> p c t i", i=4),
+                    in_=raw[g][:, :, scalar_cols:].rearrange("p t (c i) -> p c t i", i=4),
                 )
 
             def quantise_by_v(g):
                 w0_codes[g] = stream.tile(
-                    [P, R], U32, tag="w0_codes", bufs=MX_RUN + 3, align_bytes=64, name="w0_codes"
+                    [P, R], U32, tag="w0_codes", bufs=MX_RUN + 4, align_bytes=64, name="w0_codes"
                 )
                 w0_scales[g] = stream.tile(
-                    [P, R], U8, tag="w0_scales", bufs=MX_RUN + 3, align_bytes=64, name="w0_scales"
+                    [P, R], U8, tag="w0_scales", bufs=MX_RUN + 4, align_bytes=64, name="w0_scales"
                 )
                 nc.vector.quantize_mx(
                     out=w0_codes[g][:].bitcast(FP8X4),
@@ -263,38 +235,138 @@ def tile_lowrankredistributor_k_kernel(tc, logits, W, out):
                     in_=by_r[g][:].rearrange("q n t -> q (n t)"),
                 )
 
-            def step(s):
-                if s < GROUPS:
+            def scalar_cols(s):
+                if s < LEAD:
+                    return 0
+                return SCALAR_COLS_L if s < LEAD + 1 + PIECES else SCALAR_COLS
+
+            def regroup_step(s):
+                if s >= LEAD and s < GROUPS:
                     load(s)
-                    regroup(s)
-                if 0 <= s - 1 < GROUPS:
+                    regroup(s, scalar_cols(s))
+
+            def first_path_step(s):
+                if s - 1 < GROUPS:
                     transpose(s - 1)
                     quantise_by_v(s - 1)
+
+            def first_matmul_step(s):
                 if (GROUPS + 1 - s) % MX_RUN == 0:
                     for g in range(max(s - 1 - MX_RUN, 0), min(s - 1, GROUPS)):
                         first_matmul(g)
-                if 0 <= s - 3 < GROUPS:
+
+            def second_path_step(s):
+                if LEAD - 1 <= s - 3 < GROUPS:
                     empty_banks(s - 3)
-                if 0 <= s - 4 < GROUPS:
+                if LEAD - 1 <= s - 4 < GROUPS:
                     quantise_by_r(s - 4)
 
             with tc.manual_schedule():
-                for s in range(GROUPS + 2):
-                    step(s)
+                for g in range(LEAD):
+                    pieces = range(g * W_EVERY, min((g + 1) * W_EVERY, PIECES))
+                    load(g)
+                    for i in pieces:
+                        load_logits(i)
+                    regroup(g, scalar_cols(g))
+                    if g < LEAD - 1:
+                        transpose(g)
+                        empty_banks(g)
+                    if g > 0:
+                        quantise_by_r(g - 1)
+                    for i in pieces:
+                        transpose_logits(i)
+                        square_logits(i)
+                        empty_logits(i)
+                        if i == pieces[0] and g < LEAD - 1:
+                            quantise_by_v(g)
 
-                nc.vector.tensor_copy(
+                mean_var = early.tile([P, 2], F32)
+                nc.vector.bn_aggr(out=mean_var[:], in_=stats[:].rearrange("p c s -> p (c s)"))
+                diagonal = early.tile([P, P], F32)
+                row_t = early.tile([P, 1], F32)
+                nc.vector.scalar_tensor_tensor(
+                    out=diagonal[:],
+                    in0=squares[:],
+                    scalar=1.0,
+                    in1=ident_f32[:],
+                    op0=ALU.mult,
+                    op1=ALU.mult,
+                    accum_out=row_t[:],
+                )
+                mean_sq = early.tile([P, 1], F32)
+                nc.vector.scalar_tensor_tensor(
+                    out=mean_sq[:],
+                    in0=mean_var[:, 0:1],
+                    scalar=mean_var[:, 0:1],
+                    in1=mean_var[:, 1:2],
+                    op0=ALU.mult,
+                    op1=ALU.add,
+                )
+                row = early.tile([P, 1], F32)
+                nc.vector.scalar_tensor_tensor(
+                    out=row[:],
+                    in0=mean_sq[:],
+                    scalar=float(PIECES * STATS),
+                    in1=row_t[:],
+                    op0=ALU.mult,
+                    op1=ALU.add,
+                )
+                l_sq_all = psum.tile([P, 1], F32, tag="small")
+                nc.tensor.matmul(out=l_sq_all[:], lhsT=ones[:], rhs=row[:], start=True, stop=True)
+                regroup_step(LEAD)
+                l_sq = early.tile([P, 1], F32)
+                nc.vector.tensor_copy(out=l_sq[:], in_=l_sq_all[:])
+                root = early.tile([P, 1], F32)
+                nc.scalar.activation(out=root[:], in_=l_sq[:], func=ACT.Sqrt)
+                first_path_step(LEAD)
+                rough = early.tile([P, 1], F32)
+                nc.vector.reciprocal(out=rough[:], in_=root[:])
+                second_path_step(LEAD)
+                regroup_step(LEAD + 1)
+                unit = early.tile([P, 1], F32)
+                nc.vector.tensor_scalar(
+                    out=unit[:],
+                    in0=rough[:],
+                    scalar1=l_sq[:, 0:1],
+                    scalar2=rough[:, 0:1],
+                    op0=ALU.mult,
+                    op1=ALU.mult,
+                )
+                step_by = early.tile([P, 1], F32)
+                nc.vector.tensor_scalar(
+                    out=step_by[:], in0=unit[:], scalar1=-0.5, scalar2=1.5, op0=ALU.mult, op1=ALU.add
+                )
+                nc.vector.tensor_mul(out=l_inv[:], in0=rough[:], in1=step_by[:])
+
+                for s in range(LEAD + 1, GROUPS + 1):
+                    if s > LEAD + 1:
+                        regroup_step(s)
+                    c = s - LEAD - 1
+                    if c < PIECES:
+                        scale_logits(c)
+                    first_path_step(s)
+                    if c < PIECES:
+                        quantise_logits(c)
+                    first_matmul_step(s)
+                    second_path_step(s)
+                    if s == LEAD + 1:
+                        nc.vector.tensor_mul(out=l_norm[:], in0=l_sq[:], in1=l_inv[:])
+
+                first_matmul_step(GROUPS + 1)
+                second_path_step(GROUPS + 1)
+                nc.scalar.copy(
                     out=h_bf[:].rearrange("b (u e) q -> b u e q", e=2),
                     in_=h_acc[:].rearrange("b (u q e) -> b u e q", u=2, e=2),
-                )
-                nc.scalar.activation(
-                    out=h_squares[:], in_=h_acc[:], func=ACT.Square, accum_out=h_sq[:, 0:1]
                 )
                 h_t = psum.tile([P, PACK, P], BF16, tag="small")
                 for t in range(PACK):
                     nc.tensor.transpose(out=h_t[:, t, :], in_=h_bf[:, t, :], identity=ident_bf[:])
-                step(GROUPS + 2)
-                nc.vector.tensor_copy(out=h_by_r[:], in_=h_t[:].rearrange("q t b -> q b t"))
-                step(GROUPS + 3)
+                nc.scalar.copy(out=h_by_r[:], in_=h_t[:].rearrange("q t b -> q b t"))
+                second_path_step(GROUPS + 2)
+                nc.scalar.activation(
+                    out=h_squares[:], in_=h_acc[:], func=ACT.Square, accum_out=h_sq[:, 0:1]
+                )
+                second_path_step(GROUPS + 3)
                 nc.vector.quantize_mx(
                     out=h_codes[:].bitcast(FP8X4),
                     scales=h_scales[:],

@@ -29,10 +29,13 @@ STATS = 512
 GRAM = (PIECE - STATS) // P
 W_EVERY = 2
 LEAD = (PIECES + W_EVERY - 1) // W_EVERY
+FIRST_CHUNK = LEAD + 2
 L_CHUNK = 4
-STORE = 1024
-SCALAR_COLS = 208
-SCALAR_COLS_L = 320
+GROUPS_PER_STORE = 2
+POST_SCALED = 3
+SCALAR_COLS = 128
+SCALAR_COLS_L = 256
+V_SQUARES = GROUPS // 2 - 1
 MX_RUN = 4
 
 
@@ -52,10 +55,20 @@ def tile_lowrankredistributor_k_kernel(tc, logits, W, out):
         nc.vector.memset(warm[:], 1.0)
         nc.scalar.activation(out=warm[:], in_=warm[:], func=ACT.Sqrt)
 
+        o_const = keep.tile([P, 1], F32)
+        nc.vector.tensor_scalar(
+            out=o_const[:],
+            in0=ones[:, 0:1],
+            scalar1=0.0,
+            scalar2=(KEEP * KEEP + ALPHA * ALPHA) / (ALPHA * ALPHA),
+            op0=ALU.mult,
+            op1=ALU.add,
+        )
+
         logits_sb = keep.tile([P, V], BF16)
         wt_codes = keep.tile([P, GROUPS, K_PASS], U32, align_bytes=64)
         wt_scales = keep.tile([P, GROUPS, K_PASS], U8, align_bytes=64)
-        l_norm = keep.tile([P, 1], F32)
+        m_scale = keep.tile([P, 1], F32)
         l_inv = keep.tile([P, 1], F32)
         h_bf = keep.tile([P, PACK, P], BF16)
         h_by_r = keep.tile([P, P, PACK], BF16, align_bytes=64)
@@ -63,7 +76,11 @@ def tile_lowrankredistributor_k_kernel(tc, logits, W, out):
         h_scales = keep.tile([P, P], U8, align_bytes=64)
         h_acc = psum.tile([P, R], F32, tag="h_acc")
         h_sq = keep.tile([P, 1], F32)
-        h_squares = keep.tile([P, R], BF16)
+        dot_scale = keep.tile([P, 1], F32)
+        mm_parts = keep.tile([P, GROUPS - V_SQUARES], F32)
+        m_stats = keep.tile([P, V_SQUARES, 6], F32)
+        mm_v = keep.tile([P, 1], F32)
+        mm_s = keep.tile([P, 1], F32)
 
         with ExitStack() as first:
             early = first.enter_context(tc.tile_pool(name="early", bufs=1))
@@ -172,10 +189,10 @@ def tile_lowrankredistributor_k_kernel(tc, logits, W, out):
 
             def quantise_by_v(g):
                 w0_codes[g] = stream.tile(
-                    [P, R], U32, tag="w0_codes", bufs=MX_RUN + 4, align_bytes=64, name="w0_codes"
+                    [P, R], U32, tag="w0_codes", bufs=MX_RUN + 3, align_bytes=64, name="w0_codes"
                 )
                 w0_scales[g] = stream.tile(
-                    [P, R], U8, tag="w0_scales", bufs=MX_RUN + 4, align_bytes=64, name="w0_scales"
+                    [P, R], U8, tag="w0_scales", bufs=MX_RUN + 3, align_bytes=64, name="w0_scales"
                 )
                 nc.vector.quantize_mx(
                     out=w0_codes[g][:].bitcast(FP8X4),
@@ -238,7 +255,7 @@ def tile_lowrankredistributor_k_kernel(tc, logits, W, out):
             def scalar_cols(s):
                 if s < LEAD:
                     return 0
-                return SCALAR_COLS_L if s < LEAD + 1 + PIECES else SCALAR_COLS
+                return SCALAR_COLS_L if s < FIRST_CHUNK + PIECES else SCALAR_COLS
 
             def regroup_step(s):
                 if s >= LEAD and s < GROUPS:
@@ -251,9 +268,16 @@ def tile_lowrankredistributor_k_kernel(tc, logits, W, out):
                     quantise_by_v(s - 1)
 
             def first_matmul_step(s):
-                if (GROUPS + 1 - s) % MX_RUN == 0:
-                    for g in range(max(s - 1 - MX_RUN, 0), min(s - 1, GROUPS)):
+                if s == GROUPS:
+                    for g in range(GROUPS - MX_RUN, GROUPS - 1):
                         first_matmul(g)
+                elif s == GROUPS + 1:
+                    first_matmul(GROUPS - 1)
+                else:
+                    for run in range(GROUPS // MX_RUN - 1):
+                        if s == max((run + 1) * MX_RUN + 1, FIRST_CHUNK + run):
+                            for g in range(run * MX_RUN, (run + 1) * MX_RUN):
+                                first_matmul(g)
 
             def second_path_step(s):
                 if LEAD - 1 <= s - 3 < GROUPS:
@@ -274,12 +298,19 @@ def tile_lowrankredistributor_k_kernel(tc, logits, W, out):
                     if g > 0:
                         quantise_by_r(g - 1)
                     for i in pieces:
-                        transpose_logits(i)
-                        square_logits(i)
+                        if g < LEAD - 1:
+                            transpose_logits(i)
+                            square_logits(i)
+                        else:
+                            square_logits(i)
+                            transpose_logits(i)
                         empty_logits(i)
                         if i == pieces[0] and g < LEAD - 1:
                             quantise_by_v(g)
 
+                regroup_step(LEAD)
+                first_path_step(LEAD)
+                second_path_step(LEAD)
                 mean_var = early.tile([P, 2], F32)
                 nc.vector.bn_aggr(out=mean_var[:], in_=stats[:].rearrange("p c s -> p (c s)"))
                 diagonal = early.tile([P, P], F32)
@@ -313,16 +344,16 @@ def tile_lowrankredistributor_k_kernel(tc, logits, W, out):
                 )
                 l_sq_all = psum.tile([P, 1], F32, tag="small")
                 nc.tensor.matmul(out=l_sq_all[:], lhsT=ones[:], rhs=row[:], start=True, stop=True)
-                regroup_step(LEAD)
+                regroup_step(LEAD + 1)
                 l_sq = early.tile([P, 1], F32)
                 nc.vector.tensor_copy(out=l_sq[:], in_=l_sq_all[:])
                 root = early.tile([P, 1], F32)
                 nc.scalar.activation(out=root[:], in_=l_sq[:], func=ACT.Sqrt)
-                first_path_step(LEAD)
+                first_path_step(LEAD + 1)
                 rough = early.tile([P, 1], F32)
                 nc.vector.reciprocal(out=rough[:], in_=root[:])
-                second_path_step(LEAD)
-                regroup_step(LEAD + 1)
+                second_path_step(LEAD + 1)
+                regroup_step(LEAD + 2)
                 unit = early.tile([P, 1], F32)
                 nc.vector.tensor_scalar(
                     out=unit[:],
@@ -338,10 +369,10 @@ def tile_lowrankredistributor_k_kernel(tc, logits, W, out):
                 )
                 nc.vector.tensor_mul(out=l_inv[:], in0=rough[:], in1=step_by[:])
 
-                for s in range(LEAD + 1, GROUPS + 1):
-                    if s > LEAD + 1:
+                for s in range(FIRST_CHUNK, GROUPS + 1):
+                    if s > FIRST_CHUNK:
                         regroup_step(s)
-                    c = s - LEAD - 1
+                    c = s - FIRST_CHUNK
                     if c < PIECES:
                         scale_logits(c)
                     first_path_step(s)
@@ -349,59 +380,92 @@ def tile_lowrankredistributor_k_kernel(tc, logits, W, out):
                         quantise_logits(c)
                     first_matmul_step(s)
                     second_path_step(s)
-                    if s == LEAD + 1:
-                        nc.vector.tensor_mul(out=l_norm[:], in0=l_sq[:], in1=l_inv[:])
+                    if s == FIRST_CHUNK:
+                        nc.vector.tensor_scalar(
+                            out=m_scale[:],
+                            in0=l_inv[:],
+                            scalar1=l_inv[:, 0:1],
+                            scalar2=(ALPHA / KEEP) * (ALPHA / KEEP),
+                            op0=ALU.mult,
+                            op1=ALU.mult,
+                        )
 
                 first_matmul_step(GROUPS + 1)
-                second_path_step(GROUPS + 1)
-                nc.scalar.copy(
+                nc.vector.tensor_copy(
                     out=h_bf[:].rearrange("b (u e) q -> b u e q", e=2),
                     in_=h_acc[:].rearrange("b (u q e) -> b u e q", u=2, e=2),
                 )
                 h_t = psum.tile([P, PACK, P], BF16, tag="small")
                 for t in range(PACK):
                     nc.tensor.transpose(out=h_t[:, t, :], in_=h_bf[:, t, :], identity=ident_bf[:])
-                nc.scalar.copy(out=h_by_r[:], in_=h_t[:].rearrange("q t b -> q b t"))
-                second_path_step(GROUPS + 2)
-                nc.scalar.activation(
-                    out=h_squares[:], in_=h_acc[:], func=ACT.Square, accum_out=h_sq[:, 0:1]
-                )
-                second_path_step(GROUPS + 3)
+                empty_banks(GROUPS - 2)
+                quantise_by_r(GROUPS - 3)
+                nc.vector.tensor_copy(out=h_by_r[:], in_=h_t[:].rearrange("q t b -> q b t"))
                 nc.vector.quantize_mx(
                     out=h_codes[:].bitcast(FP8X4),
                     scales=h_scales[:],
                     in_=h_by_r[:].rearrange("q b t -> q (b t)"),
                 )
+                quantise_by_r(GROUPS - 2)
+                empty_banks(GROUPS - 1)
+                junk = stream.tile([P, R], BF16, tag="junk", bufs=2)
+                nc.scalar.activation(
+                    out=junk[:], in_=h_acc[:], func=ACT.Square, accum_out=h_sq[:, 0:1]
+                )
+
+                def minted_bank(g):
+                    bank = psum.tile([P, K_PASS], F32, tag="bank", bufs=6)
+                    nc.tensor.matmul_mx(
+                        out=bank[:],
+                        lhsT=h_codes[:].bitcast(FP8X4),
+                        lhsT_scale=h_scales[:],
+                        rhs=wt_codes[:, g, :].bitcast(FP8X4),
+                        rhs_scale=wt_scales[:, g, :],
+                        start=True,
+                        stop=True,
+                    )
+                    return bank
+
+                for g in range(GROUPS):
+                    bank = minted_bank(g)
+                    if g % 2 == 1 and g // 2 < V_SQUARES:
+                        nc.vector.bn_stats(out=m_stats[:, g // 2, :], in_=bank[:])
+                    else:
+                        n = g - min((g + 1) // 2, V_SQUARES)
+                        junk = stream.tile([P, R], BF16, tag="junk", bufs=2)
+                        nc.scalar.activation(
+                            out=junk[:],
+                            in_=bank[:],
+                            func=ACT.Square,
+                            accum_out=mm_parts[:, n : n + 1],
+                        )
+                    if g == 1:
+                        quantise_by_r(GROUPS - 1)
+                    if g == 3:
+                        h_sq_all = psum.tile([P, 1], F32, tag="small")
+                        nc.tensor.matmul(
+                            out=h_sq_all[:], lhsT=ones[:], rhs=h_sq[:], start=True, stop=True
+                        )
+                    if g == 5:
+                        nc.vector.tensor_scalar(
+                            out=dot_scale[:],
+                            in0=h_sq_all[:],
+                            scalar1=l_inv[:, 0:1],
+                            scalar2=2.0,
+                            op0=ALU.mult,
+                            op1=ALU.mult,
+                        )
 
         tail = ctx.enter_context(tc.tile_pool(name="tail", bufs=1, reuse_waits="tile"))
+        ctx.enter_context(tc.manual_schedule())
 
-        def minted_bank(g):
-            bank = psum.tile([P, K_PASS], F32, tag="bank", bufs=6)
-            nc.tensor.matmul_mx(
-                out=bank[:],
-                lhsT=h_codes[:].bitcast(FP8X4),
-                lhsT_scale=h_scales[:],
-                rhs=wt_codes[:, g, :].bitcast(FP8X4),
-                rhs_scale=wt_scales[:, g, :],
-                start=True,
-                stop=True,
-            )
-            return bank
-
-        mm_parts = tail.tile([P, GROUPS // 2], F32)
-        m_stats = tail.tile([P, GROUPS // 2, 6], F32)
-        for g in range(GROUPS):
-            bank = minted_bank(g)
-            if g % 2 == 0:
-                junk_s = tail.tile([P, K_PASS], BF16, tag="junk_s", bufs=4)
-                nc.scalar.activation(
-                    out=junk_s[:],
-                    in_=bank[:],
-                    func=ACT.Square,
-                    accum_out=mm_parts[:, g // 2 : g // 2 + 1],
-                )
-            else:
-                nc.vector.bn_stats(out=m_stats[:, g // 2, :], in_=bank[:])
+        stores = [range(0, 1), range(1, 2)]
+        stores += [range(g, g + GROUPS_PER_STORE) for g in range(2, GROUPS - 2, GROUPS_PER_STORE)]
+        stores += [range(GROUPS - 2, GROUPS - 1), range(GROUPS - 1, GROUPS)]
+        ahead = {}
+        for k in range(POST_SCALED):
+            for g in stores[k]:
+                ahead[g] = minted_bank(g)
 
         m_mean_var = tail.tile([P, 2], F32)
         nc.vector.bn_aggr(out=m_mean_var[:], in_=m_stats[:].rearrange("p c s -> p (c s)"))
@@ -414,74 +478,66 @@ def tile_lowrankredistributor_k_kernel(tc, logits, W, out):
             op0=ALU.mult,
             op1=ALU.add,
         )
-        mm_row = tail.tile([P, 1], F32)
-        nc.vector.tensor_reduce(out=mm_row[:], in_=mm_parts[:], axis=AXIS.X, op=ALU.add)
-        sums = tail.tile([P, 2], F32)
-        nc.vector.scalar_tensor_tensor(
-            out=sums[:, 0:1],
-            in0=m_mean_sq[:],
-            scalar=float(V // 2),
-            in1=mm_row[:],
-            op0=ALU.mult,
-            op1=ALU.add,
+        nc.vector.tensor_scalar_mul(mm_v[:], m_mean_sq[:], float(V_SQUARES * K_PASS))
+        nc.vector.tensor_reduce(out=mm_s[:], in_=mm_parts[:], axis=AXIS.X, op=ALU.add)
+        mm_all = psum.tile([P, 1], F32, tag="small")
+        nc.tensor.matmul(out=mm_all[:], lhsT=ones[:], rhs=mm_v[:], start=True, stop=False)
+        nc.tensor.matmul(out=mm_all[:], lhsT=ones[:], rhs=mm_s[:], start=False, stop=True)
+        inv_ratio = tail.tile([P, 1], F32)
+        nc.scalar.activation(
+            out=inv_ratio[:], in_=mm_all[:], func=ACT.Sqrt, scale=m_scale[:, 0:1]
         )
-        nc.vector.tensor_copy(out=sums[:, 1:2], in_=h_sq[:])
-        sums_all = psum.tile([P, 2], F32, tag="small")
-        nc.tensor.matmul(out=sums_all[:], lhsT=ones[:], rhs=sums[:], start=True, stop=True)
-        m_norm = tail.tile([P, 1], F32)
-        nc.scalar.activation(out=m_norm[:], in_=sums_all[:, 0:1], func=ACT.Sqrt)
-        m_inv = tail.tile([P, 1], F32)
-        nc.vector.reciprocal(out=m_inv[:], in_=m_norm[:])
         ratio = tail.tile([P, 1], F32)
-        nc.vector.tensor_scalar(
-            out=ratio[:],
-            in0=m_inv[:],
-            scalar1=l_norm[:, 0:1],
-            scalar2=KEEP / ALPHA,
-            op0=ALU.mult,
-            op1=ALU.mult,
-        )
-        cosine = tail.tile([P, 1], F32)
-        nc.vector.tensor_mul(out=cosine[:], in0=sums_all[:, 1:2], in1=m_inv[:])
-        o_sq = tail.tile([P, 1], F32)
-        nc.vector.tensor_scalar(
-            out=o_sq[:],
-            in0=cosine[:],
-            scalar1=2.0 * KEEP / ALPHA,
-            scalar2=(KEEP * KEEP + ALPHA * ALPHA) / (ALPHA * ALPHA),
-            op0=ALU.mult,
-            op1=ALU.add,
-        )
+        nc.vector.reciprocal(out=ratio[:], in_=inv_ratio[:])
         o_norm = tail.tile([P, 1], F32)
-        nc.scalar.activation(out=o_norm[:], in_=o_sq[:], func=ACT.Sqrt)
+        nc.scalar.activation(
+            out=o_norm[:],
+            in_=ratio[:],
+            func=ACT.Sqrt,
+            scale=dot_scale[:, 0:1],
+            bias=o_const[:, 0:1],
+        )
         c_l = tail.tile([P, 1], F32)
-        nc.vector.reciprocal(out=c_l[:], in_=o_norm[:])
+        c_m = tail.tile([P, 1], F32)
 
-        per_store = STORE // K_PASS
-        for k in range(V // STORE):
-            result = tail.tile([P, STORE], F32, tag="result", bufs=6)
-            for j in range(per_store):
-                g = k * per_store + j
-                bank = minted_bank(g)
-                nc.vector.scalar_tensor_tensor(
-                    out=result[:, j * K_PASS : (j + 1) * K_PASS],
-                    in0=bank[:],
-                    scalar=ratio[:, 0:1],
-                    in1=logits_sb[:, g * K_PASS : (g + 1) * K_PASS],
-                    op0=ALU.mult,
-                    op1=ALU.add,
-                )
-            if k % 3 == 1:
+        def times_c_l(k, result, source):
+            if k % 3 == 2:
                 nc.gpsimd.tensor_scalar(
-                    out=result[:],
-                    in0=result[:],
+                    out=result,
+                    in0=source,
                     scalar1=c_l[:, 0:1],
                     scalar2=0.0,
                     op0=ALU.mult,
                     op1=ALU.add,
                 )
             else:
-                nc.scalar.activation(
-                    out=result[:], in_=result[:], func=ACT.Copy, scale=c_l[:, 0:1]
+                nc.scalar.activation(out=result, in_=source, func=ACT.Copy, scale=c_l[:, 0:1])
+
+        for k, groups in enumerate(stores):
+            width = len(groups) * K_PASS
+            cols = slice(groups[0] * K_PASS, groups[0] * K_PASS + width)
+            result = tail.tile([P, GROUPS_PER_STORE * K_PASS], F32, tag="result", bufs=16)
+            if k >= POST_SCALED:
+                times_c_l(k, result[:, :width], logits_sb[:, cols])
+            for j, g in enumerate(groups):
+                part = result[:, j * K_PASS : (j + 1) * K_PASS]
+                bank = ahead[g] if g in ahead else minted_bank(g)
+                if k < POST_SCALED:
+                    term = logits_sb[:, g * K_PASS : (g + 1) * K_PASS]
+                else:
+                    term = part
+                nc.vector.scalar_tensor_tensor(
+                    out=part,
+                    in0=bank[:],
+                    scalar=ratio[:, 0:1] if k < POST_SCALED else c_m[:, 0:1],
+                    in1=term,
+                    op0=ALU.mult,
+                    op1=ALU.add,
                 )
-            nc.sync.dma_start(out=out[:, k * STORE : (k + 1) * STORE], in_=result[:])
+            if k == 0:
+                nc.vector.reciprocal(out=c_l[:], in_=o_norm[:])
+            if k == 1:
+                nc.vector.tensor_mul(out=c_m[:], in0=c_l[:], in1=ratio[:])
+            if k < POST_SCALED:
+                times_c_l(k, result[:, :width], result[:, :width])
+            nc.sync.dma_start(out=out[:, cols], in_=result[:, :width])

@@ -27,15 +27,15 @@ PIECE = 2048
 PIECES = V // PIECE
 STATS = 512
 GRAM = (PIECE - STATS) // P
-W_EVERY = 2
-LEAD = (PIECES + W_EVERY - 1) // W_EVERY
+LEAD = PIECES
 FIRST_CHUNK = LEAD + 2
-L_CHUNK = 4
+L_CHUNK = PIECE // K_PASS
 GROUPS_PER_STORE = 2
 POST_SCALED = 3
-SCALAR_COLS = 128
-SCALAR_COLS_L = 256
+SCALAR_COLS = 208
+SCALAR_COLS_HEAD = 288
 V_SQUARES = GROUPS // 2 - 1
+W0_BUFS = FIRST_CHUNK + 1
 MX_RUN = 4
 
 
@@ -88,17 +88,11 @@ def tile_lowrankredistributor_k_kernel(tc, logits, W, out):
 
             stats = early.tile([P, PIECES, 6], F32)
             squares = psum.tile([P, P], F32, tag="small")
-            lt = early.tile([P, GROUPS, P, PACK], BF16, align_bytes=64)
-            lt_words = (
-                lt[:]
-                .rearrange("p g b t -> p (g b t)")
-                .bitcast(F32)
-                .rearrange("p (g b u) -> p g b u", b=P, u=2)
-            )
             logit_words = logits_sb[:].bitcast(F32)
             l_codes = early.tile([P, GROUPS, P], U32, align_bytes=64)
             l_scales = early.tile([P, GROUPS, P], U8, align_bytes=64)
             l_banks = {}
+            lt = {}
 
             def load_logits(i):
                 cols = slice(i * PIECE, (i + 1) * PIECE)
@@ -133,20 +127,24 @@ def tile_lowrankredistributor_k_kernel(tc, logits, W, out):
                     l_banks[i].append(bank)
 
             def empty_logits(i):
+                lt[i] = stream.tile([P, L_CHUNK, P, PACK], BF16, tag="lt", align_bytes=64, name="lt")
+                lt_words = (
+                    lt[i][:]
+                    .rearrange("p g b t -> p (g b t)")
+                    .bitcast(F32)
+                    .rearrange("p (g b u) -> p g b u", b=P, u=2)
+                )
                 for pair in range(2):
-                    g0 = i * PIECE // K_PASS + 2 * pair
                     nc.scalar.copy(
-                        out=lt_words[:, g0 : g0 + 2, :, :],
+                        out=lt_words[:, 2 * pair : 2 * pair + 2, :, :],
                         in_=l_banks[i][pair][:].rearrange("p g u b -> p g b u"),
                     )
 
-            def lt_chunk(c):
-                return lt[:, c * L_CHUNK : (c + 1) * L_CHUNK].rearrange("p g b t -> p (g b t)")
-
             def scale_logits(c):
+                chunk = lt[c][:].rearrange("p g b t -> p (g b t)")
                 nc.vector.tensor_scalar(
-                    out=lt_chunk(c),
-                    in0=lt_chunk(c),
+                    out=chunk,
+                    in0=chunk,
                     scalar1=l_inv[:, 0:1],
                     scalar2=None,
                     op0=ALU.mult,
@@ -157,7 +155,7 @@ def tile_lowrankredistributor_k_kernel(tc, logits, W, out):
                 nc.vector.quantize_mx(
                     out=l_codes[:, gs, :].rearrange("p g b -> p (g b)").bitcast(FP8X4),
                     scales=l_scales[:, gs, :].rearrange("p g b -> p (g b)"),
-                    in_=lt_chunk(c),
+                    in_=lt[c][:].rearrange("p g b t -> p (g b t)"),
                 )
 
             w_rows = W.rearrange("(c p e) r -> p c (e r)", p=P, e=2)
@@ -177,11 +175,10 @@ def tile_lowrankredistributor_k_kernel(tc, logits, W, out):
 
             def regroup(g, scalar_cols):
                 by_v[g] = stream.tile([P, R, PACK], BF16, tag="by_v", align_bytes=64, name="by_v")
-                if scalar_cols > 0:
-                    nc.scalar.copy(
-                        out=by_v[g][:, :scalar_cols, :].rearrange("p (c i) t -> p c t i", i=4),
-                        in_=raw[g][:, :, :scalar_cols].rearrange("p t (c i) -> p c t i", i=4),
-                    )
+                nc.scalar.copy(
+                    out=by_v[g][:, :scalar_cols, :].rearrange("p (c i) t -> p c t i", i=4),
+                    in_=raw[g][:, :, :scalar_cols].rearrange("p t (c i) -> p c t i", i=4),
+                )
                 nc.vector.tensor_copy(
                     out=by_v[g][:, scalar_cols:, :].rearrange("p (c i) t -> p c t i", i=4),
                     in_=raw[g][:, :, scalar_cols:].rearrange("p t (c i) -> p c t i", i=4),
@@ -189,10 +186,10 @@ def tile_lowrankredistributor_k_kernel(tc, logits, W, out):
 
             def quantise_by_v(g):
                 w0_codes[g] = stream.tile(
-                    [P, R], U32, tag="w0_codes", bufs=MX_RUN + 3, align_bytes=64, name="w0_codes"
+                    [P, R], U32, tag="w0_codes", bufs=W0_BUFS, align_bytes=64, name="w0_codes"
                 )
                 w0_scales[g] = stream.tile(
-                    [P, R], U8, tag="w0_scales", bufs=MX_RUN + 3, align_bytes=64, name="w0_scales"
+                    [P, R], U8, tag="w0_scales", bufs=W0_BUFS, align_bytes=64, name="w0_scales"
                 )
                 nc.vector.quantize_mx(
                     out=w0_codes[g][:].bitcast(FP8X4),
@@ -252,20 +249,21 @@ def tile_lowrankredistributor_k_kernel(tc, logits, W, out):
                     in_=by_r[g][:].rearrange("q n t -> q (n t)"),
                 )
 
-            def scalar_cols(s):
-                if s < LEAD:
-                    return 0
-                return SCALAR_COLS_L if s < FIRST_CHUNK + PIECES else SCALAR_COLS
-
             def regroup_step(s):
-                if s >= LEAD and s < GROUPS:
+                if s < GROUPS:
                     load(s)
-                    regroup(s, scalar_cols(s))
+                    regroup(s, SCALAR_COLS_HEAD if s < LEAD else SCALAR_COLS)
 
             def first_path_step(s):
-                if s - 1 < GROUPS:
+                if 0 <= s - 1 < GROUPS:
                     transpose(s - 1)
                     quantise_by_v(s - 1)
+
+            def logits_step(s):
+                if 0 <= s + 2 - FIRST_CHUNK < PIECES:
+                    transpose_logits(s + 2 - FIRST_CHUNK)
+                if 0 <= s + 1 - FIRST_CHUNK < PIECES:
+                    empty_logits(s + 1 - FIRST_CHUNK)
 
             def first_matmul_step(s):
                 if s == GROUPS:
@@ -280,36 +278,22 @@ def tile_lowrankredistributor_k_kernel(tc, logits, W, out):
                                 first_matmul(g)
 
             def second_path_step(s):
-                if LEAD - 1 <= s - 3 < GROUPS:
-                    empty_banks(s - 3)
-                if LEAD - 1 <= s - 4 < GROUPS:
-                    quantise_by_r(s - 4)
+                if 0 <= s - 2 < GROUPS:
+                    empty_banks(s - 2)
+                if 0 <= s - 3 < GROUPS:
+                    quantise_by_r(s - 3)
 
             with tc.manual_schedule():
-                for g in range(LEAD):
-                    pieces = range(g * W_EVERY, min((g + 1) * W_EVERY, PIECES))
-                    load(g)
-                    for i in pieces:
-                        load_logits(i)
-                    regroup(g, scalar_cols(g))
-                    if g < LEAD - 1:
-                        transpose(g)
-                        empty_banks(g)
-                    if g > 0:
-                        quantise_by_r(g - 1)
-                    for i in pieces:
-                        if g < LEAD - 1:
-                            transpose_logits(i)
-                            square_logits(i)
-                        else:
-                            square_logits(i)
-                            transpose_logits(i)
-                        empty_logits(i)
-                        if i == pieces[0] and g < LEAD - 1:
-                            quantise_by_v(g)
+                for s in range(LEAD):
+                    regroup_step(s)
+                    load_logits(s)
+                    first_path_step(s)
+                    second_path_step(s)
+                    square_logits(s)
 
                 regroup_step(LEAD)
                 first_path_step(LEAD)
+                logits_step(LEAD)
                 second_path_step(LEAD)
                 mean_var = early.tile([P, 2], F32)
                 nc.vector.bn_aggr(out=mean_var[:], in_=stats[:].rearrange("p c s -> p (c s)"))
@@ -352,6 +336,7 @@ def tile_lowrankredistributor_k_kernel(tc, logits, W, out):
                 first_path_step(LEAD + 1)
                 rough = early.tile([P, 1], F32)
                 nc.vector.reciprocal(out=rough[:], in_=root[:])
+                logits_step(LEAD + 1)
                 second_path_step(LEAD + 1)
                 regroup_step(LEAD + 2)
                 unit = early.tile([P, 1], F32)
@@ -379,6 +364,7 @@ def tile_lowrankredistributor_k_kernel(tc, logits, W, out):
                     if c < PIECES:
                         quantise_logits(c)
                     first_matmul_step(s)
+                    logits_step(s)
                     second_path_step(s)
                     if s == FIRST_CHUNK:
                         nc.vector.tensor_scalar(
@@ -391,6 +377,7 @@ def tile_lowrankredistributor_k_kernel(tc, logits, W, out):
                         )
 
                 first_matmul_step(GROUPS + 1)
+                empty_banks(GROUPS - 1)
                 nc.vector.tensor_copy(
                     out=h_bf[:].rearrange("b (u e) q -> b u e q", e=2),
                     in_=h_acc[:].rearrange("b (u q e) -> b u e q", u=2, e=2),
@@ -398,16 +385,13 @@ def tile_lowrankredistributor_k_kernel(tc, logits, W, out):
                 h_t = psum.tile([P, PACK, P], BF16, tag="small")
                 for t in range(PACK):
                     nc.tensor.transpose(out=h_t[:, t, :], in_=h_bf[:, t, :], identity=ident_bf[:])
-                empty_banks(GROUPS - 2)
-                quantise_by_r(GROUPS - 3)
+                quantise_by_r(GROUPS - 2)
                 nc.vector.tensor_copy(out=h_by_r[:], in_=h_t[:].rearrange("q t b -> q b t"))
                 nc.vector.quantize_mx(
                     out=h_codes[:].bitcast(FP8X4),
                     scales=h_scales[:],
                     in_=h_by_r[:].rearrange("q b t -> q (b t)"),
                 )
-                quantise_by_r(GROUPS - 2)
-                empty_banks(GROUPS - 1)
                 junk = stream.tile([P, R], BF16, tag="junk", bufs=2)
                 nc.scalar.activation(
                     out=junk[:], in_=h_acc[:], func=ACT.Square, accum_out=h_sq[:, 0:1]

@@ -25,15 +25,14 @@ FLOPS = 2 * 2 * P * V * R
 
 PIECE = 2048
 PIECES = V // PIECE
-STATS = 512
-GRAM = (PIECE - STATS) // P
+SQUARES = 512
+GRAM = (PIECE - SQUARES) // P
 LEAD = PIECES
 FIRST_CHUNK = LEAD + 2
 L_CHUNK = PIECE // K_PASS
-GROUPS_PER_STORE = 2
-POST_SCALED = 3
-SCALAR_COLS = 208
-SCALAR_COLS_HEAD = 288
+POST_SCALED = 4
+SCALAR_COLS = 192
+SCALAR_COLS_HEAD = 96
 V_SQUARES = GROUPS // 2 - 1
 W0_BUFS = FIRST_CHUNK + 1
 MX_RUN = 4
@@ -53,7 +52,7 @@ def tile_lowrankredistributor_k_kernel(tc, logits, W, out):
         nc.vector.memset(ones[:], 1.0)
         warm = keep.tile([P, 1], F32)
         nc.vector.memset(warm[:], 1.0)
-        nc.scalar.activation(out=warm[:], in_=warm[:], func=ACT.Sqrt)
+        nc.scalar.activation(out=warm[:], in_=warm[:], func=ACT.Abs_reciprocal_sqrt)
 
         o_const = keep.tile([P, 1], F32)
         nc.vector.tensor_scalar(
@@ -86,7 +85,7 @@ def tile_lowrankredistributor_k_kernel(tc, logits, W, out):
             early = first.enter_context(tc.tile_pool(name="early", bufs=1))
             stream = first.enter_context(tc.tile_pool(name="stream", bufs=3))
 
-            stats = early.tile([P, PIECES, 6], F32)
+            sq_parts = early.tile([P, PIECES], F32)
             squares = psum.tile([P, P], F32, tag="small")
             logit_words = logits_sb[:].bitcast(F32)
             l_codes = early.tile([P, GROUPS, P], U32, align_bytes=64)
@@ -108,8 +107,12 @@ def tile_lowrankredistributor_k_kernel(tc, logits, W, out):
                         start=(i == 0 and j == 0),
                         stop=(i == PIECES - 1 and j == GRAM - 1),
                     )
-                nc.vector.bn_stats(
-                    out=stats[:, i, :], in_=logits_sb[:, (i + 1) * PIECE - STATS : (i + 1) * PIECE]
+                junk = stream.tile([P, R], BF16, tag="junk", bufs=2)
+                nc.scalar.activation(
+                    out=junk[:, :SQUARES],
+                    in_=logits_sb[:, (i + 1) * PIECE - SQUARES : (i + 1) * PIECE],
+                    func=ACT.Square,
+                    accum_out=sq_parts[:, i : i + 1],
                 )
 
             def transpose_logits(i):
@@ -295,8 +298,8 @@ def tile_lowrankredistributor_k_kernel(tc, logits, W, out):
                 first_path_step(LEAD)
                 logits_step(LEAD)
                 second_path_step(LEAD)
-                mean_var = early.tile([P, 2], F32)
-                nc.vector.bn_aggr(out=mean_var[:], in_=stats[:].rearrange("p c s -> p (c s)"))
+                row_s = early.tile([P, 1], F32)
+                nc.vector.tensor_reduce(out=row_s[:], in_=sq_parts[:], axis=AXIS.X, op=ALU.add)
                 diagonal = early.tile([P, P], F32)
                 row_t = early.tile([P, 1], F32)
                 nc.vector.scalar_tensor_tensor(
@@ -308,34 +311,16 @@ def tile_lowrankredistributor_k_kernel(tc, logits, W, out):
                     op1=ALU.mult,
                     accum_out=row_t[:],
                 )
-                mean_sq = early.tile([P, 1], F32)
-                nc.vector.scalar_tensor_tensor(
-                    out=mean_sq[:],
-                    in0=mean_var[:, 0:1],
-                    scalar=mean_var[:, 0:1],
-                    in1=mean_var[:, 1:2],
-                    op0=ALU.mult,
-                    op1=ALU.add,
-                )
                 row = early.tile([P, 1], F32)
-                nc.vector.scalar_tensor_tensor(
-                    out=row[:],
-                    in0=mean_sq[:],
-                    scalar=float(PIECES * STATS),
-                    in1=row_t[:],
-                    op0=ALU.mult,
-                    op1=ALU.add,
-                )
+                nc.vector.tensor_add(out=row[:], in0=row_s[:], in1=row_t[:])
                 l_sq_all = psum.tile([P, 1], F32, tag="small")
                 nc.tensor.matmul(out=l_sq_all[:], lhsT=ones[:], rhs=row[:], start=True, stop=True)
                 regroup_step(LEAD + 1)
                 l_sq = early.tile([P, 1], F32)
                 nc.vector.tensor_copy(out=l_sq[:], in_=l_sq_all[:])
-                root = early.tile([P, 1], F32)
-                nc.scalar.activation(out=root[:], in_=l_sq[:], func=ACT.Sqrt)
-                first_path_step(LEAD + 1)
                 rough = early.tile([P, 1], F32)
-                nc.vector.reciprocal(out=rough[:], in_=root[:])
+                nc.scalar.activation(out=rough[:], in_=l_sq[:], func=ACT.Abs_reciprocal_sqrt)
+                first_path_step(LEAD + 1)
                 logits_step(LEAD + 1)
                 second_path_step(LEAD + 1)
                 regroup_step(LEAD + 2)
@@ -392,6 +377,7 @@ def tile_lowrankredistributor_k_kernel(tc, logits, W, out):
                     scales=h_scales[:],
                     in_=h_by_r[:].rearrange("q b t -> q (b t)"),
                 )
+                quantise_by_r(GROUPS - 1)
                 junk = stream.tile([P, R], BF16, tag="junk", bufs=2)
                 nc.scalar.activation(
                     out=junk[:], in_=h_acc[:], func=ACT.Square, accum_out=h_sq[:, 0:1]
@@ -423,8 +409,6 @@ def tile_lowrankredistributor_k_kernel(tc, logits, W, out):
                             func=ACT.Square,
                             accum_out=mm_parts[:, n : n + 1],
                         )
-                    if g == 1:
-                        quantise_by_r(GROUPS - 1)
                     if g == 3:
                         h_sq_all = psum.tile([P, 1], F32, tag="small")
                         nc.tensor.matmul(
@@ -443,9 +427,9 @@ def tile_lowrankredistributor_k_kernel(tc, logits, W, out):
         tail = ctx.enter_context(tc.tile_pool(name="tail", bufs=1, reuse_waits="tile"))
         ctx.enter_context(tc.manual_schedule())
 
-        stores = [range(0, 1), range(1, 2)]
-        stores += [range(g, g + GROUPS_PER_STORE) for g in range(2, GROUPS - 2, GROUPS_PER_STORE)]
-        stores += [range(GROUPS - 2, GROUPS - 1), range(GROUPS - 1, GROUPS)]
+        stores = [range(g, g + 1) for g in range(POST_SCALED)]
+        stores += [range(g, g + 2) for g in range(POST_SCALED, GROUPS - 2, 2)]
+        stores += [range(g, g + 1) for g in range(GROUPS - 2, GROUPS)]
         ahead = {}
         for k in range(POST_SCALED):
             for g in stores[k]:
@@ -467,25 +451,22 @@ def tile_lowrankredistributor_k_kernel(tc, logits, W, out):
         mm_all = psum.tile([P, 1], F32, tag="small")
         nc.tensor.matmul(out=mm_all[:], lhsT=ones[:], rhs=mm_v[:], start=True, stop=False)
         nc.tensor.matmul(out=mm_all[:], lhsT=ones[:], rhs=mm_s[:], start=False, stop=True)
-        inv_ratio = tail.tile([P, 1], F32)
-        nc.scalar.activation(
-            out=inv_ratio[:], in_=mm_all[:], func=ACT.Sqrt, scale=m_scale[:, 0:1]
-        )
         ratio = tail.tile([P, 1], F32)
-        nc.vector.reciprocal(out=ratio[:], in_=inv_ratio[:])
-        o_norm = tail.tile([P, 1], F32)
         nc.scalar.activation(
-            out=o_norm[:],
+            out=ratio[:], in_=mm_all[:], func=ACT.Abs_reciprocal_sqrt, scale=m_scale[:, 0:1]
+        )
+        c_l = tail.tile([P, 1], F32)
+        nc.scalar.activation(
+            out=c_l[:],
             in_=ratio[:],
-            func=ACT.Sqrt,
+            func=ACT.Abs_reciprocal_sqrt,
             scale=dot_scale[:, 0:1],
             bias=o_const[:, 0:1],
         )
-        c_l = tail.tile([P, 1], F32)
         c_m = tail.tile([P, 1], F32)
 
         def times_c_l(k, result, source):
-            if k % 3 == 2:
+            if k == POST_SCALED or (k > POST_SCALED and k % 3 == 2):
                 nc.gpsimd.tensor_scalar(
                     out=result,
                     in0=source,
@@ -497,12 +478,27 @@ def tile_lowrankredistributor_k_kernel(tc, logits, W, out):
             else:
                 nc.scalar.activation(out=result, in_=source, func=ACT.Copy, scale=c_l[:, 0:1])
 
+        results = {}
+
+        def scale_ahead(k):
+            width = len(stores[k]) * K_PASS
+            g0 = stores[k][0]
+            results[k] = tail.tile(
+                [P, 2 * K_PASS], F32, tag="result", bufs=16, name="result"
+            )
+            if k >= POST_SCALED:
+                times_c_l(
+                    k, results[k][:, :width], logits_sb[:, g0 * K_PASS : g0 * K_PASS + width]
+                )
+
+        scale_ahead(0)
+        scale_ahead(1)
         for k, groups in enumerate(stores):
             width = len(groups) * K_PASS
             cols = slice(groups[0] * K_PASS, groups[0] * K_PASS + width)
-            result = tail.tile([P, GROUPS_PER_STORE * K_PASS], F32, tag="result", bufs=16)
-            if k >= POST_SCALED:
-                times_c_l(k, result[:, :width], logits_sb[:, cols])
+            if k + 2 < len(stores):
+                scale_ahead(k + 2)
+            result = results[k]
             for j, g in enumerate(groups):
                 part = result[:, j * K_PASS : (j + 1) * K_PASS]
                 bank = ahead[g] if g in ahead else minted_bank(g)
@@ -518,8 +514,6 @@ def tile_lowrankredistributor_k_kernel(tc, logits, W, out):
                     op0=ALU.mult,
                     op1=ALU.add,
                 )
-            if k == 0:
-                nc.vector.reciprocal(out=c_l[:], in_=o_norm[:])
             if k == 1:
                 nc.vector.tensor_mul(out=c_m[:], in0=c_l[:], in1=ratio[:])
             if k < POST_SCALED:

@@ -27,14 +27,14 @@ PIECE = 2048
 PIECES = V // PIECE
 SQUARES = 512
 GRAM = (PIECE - SQUARES) // P
-LEAD = PIECES
+LEAD = PIECES // 2 * 3
 FIRST_CHUNK = LEAD + 2
 L_CHUNK = PIECE // K_PASS
 POST_SCALED = 4
 SCALAR_COLS = 192
-SCALAR_COLS_HEAD = 96
+SCALAR_COLS_HEAD = 128
 V_SQUARES = GROUPS // 2 - 1
-W0_BUFS = FIRST_CHUNK + 1
+PARKED = FIRST_CHUNK
 MX_RUN = 4
 
 
@@ -170,7 +170,7 @@ def tile_lowrankredistributor_k_kernel(tc, logits, W, out):
             w0_scales = {}
 
             def load(g):
-                raw[g] = stream.tile([P, PACK, R], BF16, tag="raw", bufs=6, name="raw")
+                raw[g] = stream.tile([P, PACK, R], BF16, tag="raw", bufs=8, name="raw")
                 nc.sync.dma_start(
                     out=raw[g][:].rearrange("p (u e) r -> p u (e r)", e=2),
                     in_=w_rows[:, 2 * g : 2 * g + 2, :],
@@ -188,15 +188,21 @@ def tile_lowrankredistributor_k_kernel(tc, logits, W, out):
                 )
 
             def quantise_by_v(g):
-                w0_codes[g] = stream.tile(
-                    [P, R], U32, tag="w0_codes", bufs=W0_BUFS, align_bytes=64, name="w0_codes"
-                )
-                w0_scales[g] = stream.tile(
-                    [P, R], U8, tag="w0_scales", bufs=W0_BUFS, align_bytes=64, name="w0_scales"
-                )
+                if g < PARKED:
+                    w0_codes[g] = wt_codes[:, GROUPS - 1 - g, :]
+                    w0_scales[g] = wt_scales[:, GROUPS - 1 - g, :]
+                else:
+                    codes = stream.tile(
+                        [P, R], U32, tag="w0_codes", bufs=MX_RUN + 3, align_bytes=64, name="w0_codes"
+                    )
+                    scales = stream.tile(
+                        [P, R], U8, tag="w0_scales", bufs=MX_RUN + 3, align_bytes=64, name="w0_scales"
+                    )
+                    w0_codes[g] = codes[:]
+                    w0_scales[g] = scales[:]
                 nc.vector.quantize_mx(
-                    out=w0_codes[g][:].bitcast(FP8X4),
-                    scales=w0_scales[g][:],
+                    out=w0_codes[g].bitcast(FP8X4),
+                    scales=w0_scales[g],
                     in_=by_v[g][:].rearrange("p r t -> p (r t)"),
                 )
 
@@ -205,8 +211,8 @@ def tile_lowrankredistributor_k_kernel(tc, logits, W, out):
                     out=h_acc[:],
                     lhsT=l_codes[:, g, :].bitcast(FP8X4),
                     lhsT_scale=l_scales[:, g, :],
-                    rhs=w0_codes[g][:].bitcast(FP8X4),
-                    rhs_scale=w0_scales[g][:],
+                    rhs=w0_codes[g].bitcast(FP8X4),
+                    rhs_scale=w0_scales[g],
                     start=(g == 0),
                     stop=(g == GROUPS - 1),
                 )
@@ -289,10 +295,12 @@ def tile_lowrankredistributor_k_kernel(tc, logits, W, out):
             with tc.manual_schedule():
                 for s in range(LEAD):
                     regroup_step(s)
-                    load_logits(s)
+                    if s % 3 > 0:
+                        load_logits(s // 3 * 2 + s % 3 - 1)
                     first_path_step(s)
                     second_path_step(s)
-                    square_logits(s)
+                    if s % 3 > 0:
+                        square_logits(s // 3 * 2 + s % 3 - 1)
 
                 regroup_step(LEAD)
                 first_path_step(LEAD)

@@ -33,7 +33,8 @@ L_CHUNK = PIECE // K_PASS
 POST_SCALED = 4
 SCALAR_COLS = 192
 SCALAR_COLS_HEAD = 128
-V_SQUARES = GROUPS // 2 - 1
+V_SQUARES = 15
+DEFERRED = 5
 PARKED = FIRST_CHUNK
 MX_RUN = 4
 
@@ -170,7 +171,7 @@ def tile_lowrankredistributor_k_kernel(tc, logits, W, out):
             w0_scales = {}
 
             def load(g):
-                raw[g] = stream.tile([P, PACK, R], BF16, tag="raw", bufs=8, name="raw")
+                raw[g] = stream.tile([P, PACK, R], BF16, tag="raw", bufs=7, name="raw")
                 nc.sync.dma_start(
                     out=raw[g][:].rearrange("p (u e) r -> p u (e r)", e=2),
                     in_=w_rows[:, 2 * g : 2 * g + 2, :],
@@ -238,7 +239,7 @@ def tile_lowrankredistributor_k_kernel(tc, logits, W, out):
 
             def empty_banks(g):
                 by_r[g] = stream.tile(
-                    [P, K_PASS, PACK], BF16, tag="by_r", align_bytes=64, name="by_r"
+                    [P, K_PASS, PACK], BF16, tag="by_r", bufs=DEFERRED, align_bytes=64, name="by_r"
                 )
                 by_r_words = (
                     by_r[g][:]
@@ -282,14 +283,14 @@ def tile_lowrankredistributor_k_kernel(tc, logits, W, out):
                     first_matmul(GROUPS - 1)
                 else:
                     for run in range(GROUPS // MX_RUN - 1):
-                        if s == max((run + 1) * MX_RUN + 1, FIRST_CHUNK + run):
+                        if s == max((run + 1) * MX_RUN + 1, FIRST_CHUNK + run + 1):
                             for g in range(run * MX_RUN, (run + 1) * MX_RUN):
                                 first_matmul(g)
 
             def second_path_step(s):
                 if 0 <= s - 2 < GROUPS:
                     empty_banks(s - 2)
-                if 0 <= s - 3 < GROUPS:
+                if 0 <= s - 3 < GROUPS - DEFERRED:
                     quantise_by_r(s - 3)
 
             with tc.manual_schedule():
@@ -306,6 +307,7 @@ def tile_lowrankredistributor_k_kernel(tc, logits, W, out):
                 first_path_step(LEAD)
                 logits_step(LEAD)
                 second_path_step(LEAD)
+                regroup_step(LEAD + 1)
                 row_s = early.tile([P, 1], F32)
                 nc.vector.tensor_reduce(out=row_s[:], in_=sq_parts[:], axis=AXIS.X, op=ALU.add)
                 diagonal = early.tile([P, P], F32)
@@ -319,17 +321,15 @@ def tile_lowrankredistributor_k_kernel(tc, logits, W, out):
                     op1=ALU.mult,
                     accum_out=row_t[:],
                 )
-                row = early.tile([P, 1], F32)
-                nc.vector.tensor_add(out=row[:], in0=row_s[:], in1=row_t[:])
                 l_sq_all = psum.tile([P, 1], F32, tag="small")
-                nc.tensor.matmul(out=l_sq_all[:], lhsT=ones[:], rhs=row[:], start=True, stop=True)
-                regroup_step(LEAD + 1)
+                nc.tensor.matmul(out=l_sq_all[:], lhsT=ones[:], rhs=row_s[:], start=True, stop=False)
+                nc.tensor.matmul(out=l_sq_all[:], lhsT=ones[:], rhs=row_t[:], start=False, stop=True)
+                first_path_step(LEAD + 1)
+                logits_step(LEAD + 1)
                 l_sq = early.tile([P, 1], F32)
                 nc.vector.tensor_copy(out=l_sq[:], in_=l_sq_all[:])
                 rough = early.tile([P, 1], F32)
-                nc.scalar.activation(out=rough[:], in_=l_sq[:], func=ACT.Abs_reciprocal_sqrt)
-                first_path_step(LEAD + 1)
-                logits_step(LEAD + 1)
+                nc.scalar.activation(out=rough[:], in_=l_sq_all[:], func=ACT.Abs_reciprocal_sqrt)
                 second_path_step(LEAD + 1)
                 regroup_step(LEAD + 2)
                 unit = early.tile([P, 1], F32)
@@ -356,8 +356,8 @@ def tile_lowrankredistributor_k_kernel(tc, logits, W, out):
                     first_path_step(s)
                     if c < PIECES:
                         quantise_logits(c)
-                    first_matmul_step(s)
                     logits_step(s)
+                    first_matmul_step(s)
                     second_path_step(s)
                     if s == FIRST_CHUNK:
                         nc.vector.tensor_scalar(
@@ -371,6 +371,7 @@ def tile_lowrankredistributor_k_kernel(tc, logits, W, out):
 
                 first_matmul_step(GROUPS + 1)
                 empty_banks(GROUPS - 1)
+                quantise_by_r(GROUPS - 5)
                 nc.vector.tensor_copy(
                     out=h_bf[:].rearrange("b (u e) q -> b u e q", e=2),
                     in_=h_acc[:].rearrange("b (u q e) -> b u e q", u=2, e=2),
@@ -378,13 +379,15 @@ def tile_lowrankredistributor_k_kernel(tc, logits, W, out):
                 h_t = psum.tile([P, PACK, P], BF16, tag="small")
                 for t in range(PACK):
                     nc.tensor.transpose(out=h_t[:, t, :], in_=h_bf[:, t, :], identity=ident_bf[:])
-                quantise_by_r(GROUPS - 2)
+                quantise_by_r(GROUPS - 4)
                 nc.vector.tensor_copy(out=h_by_r[:], in_=h_t[:].rearrange("q t b -> q b t"))
                 nc.vector.quantize_mx(
                     out=h_codes[:].bitcast(FP8X4),
                     scales=h_scales[:],
                     in_=h_by_r[:].rearrange("q b t -> q (b t)"),
                 )
+                quantise_by_r(GROUPS - 3)
+                quantise_by_r(GROUPS - 2)
                 quantise_by_r(GROUPS - 1)
                 junk = stream.tile([P, R], BF16, tag="junk", bufs=2)
                 nc.scalar.activation(
@@ -404,12 +407,14 @@ def tile_lowrankredistributor_k_kernel(tc, logits, W, out):
                     )
                     return bank
 
+                by_vector = list(range(1, GROUPS - 2, 2))
+                by_scalar = [g for g in range(GROUPS) if g not in by_vector]
                 for g in range(GROUPS):
                     bank = minted_bank(g)
-                    if g % 2 == 1 and g // 2 < V_SQUARES:
-                        nc.vector.bn_stats(out=m_stats[:, g // 2, :], in_=bank[:])
+                    if g in by_vector:
+                        nc.vector.bn_stats(out=m_stats[:, by_vector.index(g), :], in_=bank[:])
                     else:
-                        n = g - min((g + 1) // 2, V_SQUARES)
+                        n = by_scalar.index(g)
                         junk = stream.tile([P, R], BF16, tag="junk", bufs=2)
                         nc.scalar.activation(
                             out=junk[:],

@@ -27,13 +27,13 @@ PIECE = 2048
 PIECES = V // PIECE
 SQUARES = 512
 GRAM = (PIECE - SQUARES) // P
-LEAD = PIECES // 2 * 3
+LEAD = PIECES // 2 * 3 + 1
 FIRST_CHUNK = LEAD + 2
 L_CHUNK = PIECE // K_PASS
 POST_SCALED = 4
-SCALAR_COLS = 192
+SCALAR_COLS = 176
 SCALAR_COLS_HEAD = 128
-V_SQUARES = 15
+V_SQUARES = 16
 DEFERRED = 5
 PARKED = FIRST_CHUNK
 MX_RUN = 4
@@ -296,12 +296,12 @@ def tile_lowrankredistributor_k_kernel(tc, logits, W, out):
             with tc.manual_schedule():
                 for s in range(LEAD):
                     regroup_step(s)
-                    if s % 3 > 0:
-                        load_logits(s // 3 * 2 + s % 3 - 1)
+                    if s >= 2 and s % 3 != 1:
+                        load_logits((s - 2) // 3 * 2 + (s - 2) % 3)
                     first_path_step(s)
                     second_path_step(s)
-                    if s % 3 > 0:
-                        square_logits(s // 3 * 2 + s % 3 - 1)
+                    if s >= 2 and s % 3 != 1:
+                        square_logits((s - 2) // 3 * 2 + (s - 2) % 3)
 
                 regroup_step(LEAD)
                 first_path_step(LEAD)
@@ -370,15 +370,31 @@ def tile_lowrankredistributor_k_kernel(tc, logits, W, out):
                         )
 
                 first_matmul_step(GROUPS + 1)
+
+                def keep_busy(count):
+                    spare = psum.tile([P, R], F32, tag="bank", bufs=6)
+                    for n in range(count):
+                        nc.tensor.matmul_mx(
+                            out=spare[:],
+                            lhsT=l_codes[:, GROUPS - 1, :].bitcast(FP8X4),
+                            lhsT_scale=l_scales[:, GROUPS - 1, :],
+                            rhs=w0_codes[GROUPS - 1].bitcast(FP8X4),
+                            rhs_scale=w0_scales[GROUPS - 1],
+                            start=True,
+                            stop=True,
+                        )
+
                 empty_banks(GROUPS - 1)
                 quantise_by_r(GROUPS - 5)
                 nc.vector.tensor_copy(
                     out=h_bf[:].rearrange("b (u e) q -> b u e q", e=2),
                     in_=h_acc[:].rearrange("b (u q e) -> b u e q", u=2, e=2),
                 )
+                keep_busy(2)
                 h_t = psum.tile([P, PACK, P], BF16, tag="small")
                 for t in range(PACK):
                     nc.tensor.transpose(out=h_t[:, t, :], in_=h_bf[:, t, :], identity=ident_bf[:])
+                keep_busy(3)
                 quantise_by_r(GROUPS - 4)
                 nc.vector.tensor_copy(out=h_by_r[:], in_=h_t[:].rearrange("q t b -> q b t"))
                 nc.vector.quantize_mx(
@@ -407,7 +423,7 @@ def tile_lowrankredistributor_k_kernel(tc, logits, W, out):
                     )
                     return bank
 
-                by_vector = list(range(1, GROUPS - 2, 2))
+                by_vector = sorted(list(range(1, GROUPS - 2, 2)) + [GROUPS // 2])
                 by_scalar = [g for g in range(GROUPS) if g not in by_vector]
                 for g in range(GROUPS):
                     bank = minted_bank(g)

@@ -180,12 +180,12 @@ def tile_lowrankredistributor_k_kernel(tc, logits, W, out):
             def regroup(g, scalar_cols):
                 by_v[g] = stream.tile([P, R, PACK], BF16, tag="by_v", align_bytes=64, name="by_v")
                 nc.scalar.copy(
-                    out=by_v[g][:, :scalar_cols, :].rearrange("p (c i) t -> p c t i", i=4),
-                    in_=raw[g][:, :, :scalar_cols].rearrange("p t (c i) -> p c t i", i=4),
+                    out=by_v[g][:, :scalar_cols, :].rearrange("p (c i) t -> p c t i", i=8),
+                    in_=raw[g][:, :, :scalar_cols].rearrange("p t (c i) -> p c t i", i=8),
                 )
                 nc.vector.tensor_copy(
-                    out=by_v[g][:, scalar_cols:, :].rearrange("p (c i) t -> p c t i", i=4),
-                    in_=raw[g][:, :, scalar_cols:].rearrange("p t (c i) -> p c t i", i=4),
+                    out=by_v[g][:, scalar_cols:, :].rearrange("p (c i) t -> p c t i", i=8),
+                    in_=raw[g][:, :, scalar_cols:].rearrange("p t (c i) -> p c t i", i=8),
                 )
 
             def quantise_by_v(g):

from contextlib import ExitStack

import concourse.mybir as mybir
from concourse.masks import make_identity

F32 = mybir.dt.float32
BF16 = mybir.dt.bfloat16
U32 = mybir.dt.uint32
U8 = mybir.dt.uint8
FP8X4 = mybir.dt.float8_e4m3fn_x4
ALU = mybir.AluOpType
ACT = mybir.ActivationFunctionType
AXIS = mybir.AxisListType

P = 128
V = 16384
R = 512
PACK = 4
K_PASS = P * PACK
GROUPS = V // K_PASS
ALPHA = 0.3
KEEP = 1.0 - ALPHA

FLOPS = 2 * 2 * P * V * R

PIECE = 2048
PIECES = V // PIECE
SQUARES = 512
GRAM = (PIECE - SQUARES) // P
LEAD = PIECES // 2 * 3 + 1
FIRST_CHUNK = LEAD + 2
L_CHUNK = PIECE // K_PASS
POST_SCALED = 4
SCALAR_COLS = 176
SCALAR_COLS_HEAD = 128
V_SQUARES = 16
DEFERRED = 5
PARKED = FIRST_CHUNK
MX_RUN = 4


def tile_lowrankredistributor_k_kernel(tc, logits, W, out):
    nc = tc.nc
    with ExitStack() as ctx:
        keep = ctx.enter_context(tc.tile_pool(name="keep", bufs=1))
        psum = ctx.enter_context(tc.psum_pool(name="psum", bufs=1))

        ident_f32 = keep.tile([P, P], F32)
        make_identity(nc, ident_f32[:])
        ident_bf = keep.tile([P, P], BF16)
        make_identity(nc, ident_bf[:])
        ones = keep.tile([P, P], F32)
        nc.vector.memset(ones[:], 1.0)
        warm = keep.tile([P, 1], F32)
        nc.vector.memset(warm[:], 1.0)
        nc.scalar.activation(out=warm[:], in_=warm[:], func=ACT.Abs_reciprocal_sqrt)

        o_const = keep.tile([P, 1], F32)
        nc.vector.tensor_scalar(
            out=o_const[:],
            in0=ones[:, 0:1],
            scalar1=0.0,
            scalar2=(KEEP * KEEP + ALPHA * ALPHA) / (ALPHA * ALPHA),
            op0=ALU.mult,
            op1=ALU.add,
        )

        logits_sb = keep.tile([P, V], BF16)
        wt_codes = keep.tile([P, GROUPS, K_PASS], U32, align_bytes=64)
        wt_scales = keep.tile([P, GROUPS, K_PASS], U8, align_bytes=64)
        m_scale = keep.tile([P, 1], F32)
        l_inv = keep.tile([P, 1], F32)
        h_bf = keep.tile([P, PACK, P], BF16)
        h_by_r = keep.tile([P, P, PACK], BF16, align_bytes=64)
        h_codes = keep.tile([P, P], U32, align_bytes=64)
        h_scales = keep.tile([P, P], U8, align_bytes=64)
        h_acc = psum.tile([P, R], F32, tag="h_acc")
        h_sq = keep.tile([P, 1], F32)
        dot_scale = keep.tile([P, 1], F32)
        mm_parts = keep.tile([P, GROUPS - V_SQUARES], F32)
        m_stats = keep.tile([P, V_SQUARES, 6], F32)
        mm_v = keep.tile([P, 1], F32)
        mm_s = keep.tile([P, 1], F32)

        with ExitStack() as first:
            early = first.enter_context(tc.tile_pool(name="early", bufs=1))
            stream = first.enter_context(tc.tile_pool(name="stream", bufs=3))

            sq_parts = early.tile([P, PIECES], F32)
            squares = psum.tile([P, P], F32, tag="small")
            logit_words = logits_sb[:].bitcast(F32)
            l_codes = early.tile([P, GROUPS, P], U32, align_bytes=64)
            l_scales = early.tile([P, GROUPS, P], U8, align_bytes=64)
            l_banks = {}
            lt = {}

            def load_logits(i):
                cols = slice(i * PIECE, (i + 1) * PIECE)
                nc.sync.dma_start(out=logits_sb[:, cols], in_=logits[:, cols])

            def square_logits(i):
                for j in range(GRAM):
                    block = logits_sb[:, i * PIECE + j * P : i * PIECE + (j + 1) * P]
                    nc.tensor.matmul(
                        out=squares[:],
                        lhsT=block,
                        rhs=block,
                        start=(i == 0 and j == 0),
                        stop=(i == PIECES - 1 and j == GRAM - 1),
                    )
                junk = stream.tile([P, R], BF16, tag="junk", bufs=2)
                nc.scalar.activation(
                    out=junk[:, :SQUARES],
                    in_=logits_sb[:, (i + 1) * PIECE - SQUARES : (i + 1) * PIECE],
                    func=ACT.Square,
                    accum_out=sq_parts[:, i : i + 1],
                )

            def transpose_logits(i):
                l_banks[i] = []
                for pair in range(2):
                    bank = psum.tile([P, 2, 2, P], F32, tag="bank", bufs=6)
                    for g2 in range(2):
                        for u in range(2):
                            w0 = i * PIECE // 2 + 256 * (2 * pair + g2) + P * u
                            nc.tensor.transpose(
                                out=bank[:, g2, u, :],
                                in_=logit_words[:, w0 : w0 + P],
                                identity=ident_f32[:],
                            )
                    l_banks[i].append(bank)

            def empty_logits(i):
                lt[i] = stream.tile([P, L_CHUNK, P, PACK], BF16, tag="lt", align_bytes=64, name="lt")
                lt_words = (
                    lt[i][:]
                    .rearrange("p g b t -> p (g b t)")
                    .bitcast(F32)
                    .rearrange("p (g b u) -> p g b u", b=P, u=2)
                )
                for pair in range(2):
                    nc.scalar.copy(
                        out=lt_words[:, 2 * pair : 2 * pair + 2, :, :],
                        in_=l_banks[i][pair][:].rearrange("p g u b -> p g b u"),
                    )

            def scale_logits(c):
                chunk = lt[c][:].rearrange("p g b t -> p (g b t)")
                nc.vector.tensor_scalar(
                    out=chunk,
                    in0=chunk,
                    scalar1=l_inv[:, 0:1],
                    scalar2=None,
                    op0=ALU.mult,
                )

            def quantise_logits(c):
                gs = slice(c * L_CHUNK, (c + 1) * L_CHUNK)
                nc.vector.quantize_mx(
                    out=l_codes[:, gs, :].rearrange("p g b -> p (g b)").bitcast(FP8X4),
                    scales=l_scales[:, gs, :].rearrange("p g b -> p (g b)"),
                    in_=lt[c][:].rearrange("p g b t -> p (g b t)"),
                )

            w_rows = W.rearrange("(c p e) r -> p c (e r)", p=P, e=2)
            raw = {}
            by_v = {}
            by_r = {}
            banks = {}
            w0_codes = {}
            w0_scales = {}

            def load(g):
                raw[g] = stream.tile([P, PACK, R], BF16, tag="raw", bufs=7, name="raw")
                nc.sync.dma_start(
                    out=raw[g][:].rearrange("p (u e) r -> p u (e r)", e=2),
                    in_=w_rows[:, 2 * g : 2 * g + 2, :],
                )

            def regroup(g, scalar_cols):
                by_v[g] = stream.tile([P, R, PACK], BF16, tag="by_v", align_bytes=64, name="by_v")
                nc.scalar.copy(
                    out=by_v[g][:, :scalar_cols, :].rearrange("p (c i) t -> p c t i", i=8),
                    in_=raw[g][:, :, :scalar_cols].rearrange("p t (c i) -> p c t i", i=8),
                )
                nc.vector.tensor_copy(
                    out=by_v[g][:, scalar_cols:, :].rearrange("p (c i) t -> p c t i", i=8),
                    in_=raw[g][:, :, scalar_cols:].rearrange("p t (c i) -> p c t i", i=8),
                )

            def quantise_by_v(g):
                if g < PARKED:
                    w0_codes[g] = wt_codes[:, GROUPS - 1 - g, :]
                    w0_scales[g] = wt_scales[:, GROUPS - 1 - g, :]
                else:
                    codes = stream.tile(
                        [P, R], U32, tag="w0_codes", bufs=MX_RUN + 3, align_bytes=64, name="w0_codes"
                    )
                    scales = stream.tile(
                        [P, R], U8, tag="w0_scales", bufs=MX_RUN + 3, align_bytes=64, name="w0_scales"
                    )
                    w0_codes[g] = codes[:]
                    w0_scales[g] = scales[:]
                nc.vector.quantize_mx(
                    out=w0_codes[g].bitcast(FP8X4),
                    scales=w0_scales[g],
                    in_=by_v[g][:].rearrange("p r t -> p (r t)"),
                )

            def first_matmul(g):
                nc.tensor.matmul_mx(
                    out=h_acc[:],
                    lhsT=l_codes[:, g, :].bitcast(FP8X4),
                    lhsT_scale=l_scales[:, g, :],
                    rhs=w0_codes[g].bitcast(FP8X4),
                    rhs_scale=w0_scales[g],
                    start=(g == 0),
                    stop=(g == GROUPS - 1),
                )

            def transpose(g):
                raw_words = (
                    raw[g][:]
                    .rearrange("p t r -> p (t r)")
                    .bitcast(F32)
                    .rearrange("p (t w) -> p t w", t=PACK)
                )
                banks[g] = []
                for a in range(2):
                    bank = psum.tile([P, 2, 2, P], F32, tag="bank", bufs=6)
                    for e in range(2):
                        for u in range(2):
                            nc.tensor.transpose(
                                out=bank[:, e, u, :],
                                in_=raw_words[:, 2 * a + e, P * u : P * u + P],
                                identity=ident_f32[:],
                            )
                    banks[g].append(bank)

            def empty_banks(g):
                by_r[g] = stream.tile(
                    [P, K_PASS, PACK], BF16, tag="by_r", bufs=DEFERRED, align_bytes=64, name="by_r"
                )
                by_r_words = (
                    by_r[g][:]
                    .rearrange("q n t -> q (n t)")
                    .bitcast(F32)
                    .rearrange("q (a p e u) -> q a p e u", a=2, e=2, u=2)
                )
                for a in range(2):
                    nc.scalar.copy(
                        out=by_r_words[:, a], in_=banks[g][a][:].rearrange("q e u p -> q p e u")
                    )

            def quantise_by_r(g):
                nc.vector.quantize_mx(
                    out=wt_codes[:, g, :].bitcast(FP8X4),
                    scales=wt_scales[:, g, :],
                    in_=by_r[g][:].rearrange("q n t -> q (n t)"),
                )

            def regroup_step(s):
                if s < GROUPS:
                    load(s)
                    regroup(s, SCALAR_COLS_HEAD if s < LEAD else SCALAR_COLS)

            def first_path_step(s):
                if 0 <= s - 1 < GROUPS:
                    transpose(s - 1)
                    quantise_by_v(s - 1)

            def logits_step(s):
                if 0 <= s + 2 - FIRST_CHUNK < PIECES:
                    transpose_logits(s + 2 - FIRST_CHUNK)
                if 0 <= s + 1 - FIRST_CHUNK < PIECES:
                    empty_logits(s + 1 - FIRST_CHUNK)

            def first_matmul_step(s):
                if s == GROUPS:
                    for g in range(GROUPS - MX_RUN, GROUPS - 1):
                        first_matmul(g)
                elif s == GROUPS + 1:
                    first_matmul(GROUPS - 1)
                else:
                    for run in range(GROUPS // MX_RUN - 1):
                        if s == max((run + 1) * MX_RUN + 1, FIRST_CHUNK + run + 1):
                            for g in range(run * MX_RUN, (run + 1) * MX_RUN):
                                first_matmul(g)

            def second_path_step(s):
                if 0 <= s - 2 < GROUPS:
                    empty_banks(s - 2)
                if 0 <= s - 3 < GROUPS - DEFERRED:
                    quantise_by_r(s - 3)

            with tc.manual_schedule():
                for s in range(LEAD):
                    regroup_step(s)
                    if s >= 2 and s % 3 != 1:
                        load_logits((s - 2) // 3 * 2 + (s - 2) % 3)
                    first_path_step(s)
                    second_path_step(s)
                    if s >= 2 and s % 3 != 1:
                        square_logits((s - 2) // 3 * 2 + (s - 2) % 3)

                regroup_step(LEAD)
                first_path_step(LEAD)
                logits_step(LEAD)
                second_path_step(LEAD)
                regroup_step(LEAD + 1)
                row_s = early.tile([P, 1], F32)
                nc.vector.tensor_reduce(out=row_s[:], in_=sq_parts[:], axis=AXIS.X, op=ALU.add)
                diagonal = early.tile([P, P], F32)
                row_t = early.tile([P, 1], F32)
                nc.vector.scalar_tensor_tensor(
                    out=diagonal[:],
                    in0=squares[:],
                    scalar=1.0,
                    in1=ident_f32[:],
                    op0=ALU.mult,
                    op1=ALU.mult,
                    accum_out=row_t[:],
                )
                l_sq_all = psum.tile([P, 1], F32, tag="small")
                nc.tensor.matmul(out=l_sq_all[:], lhsT=ones[:], rhs=row_s[:], start=True, stop=False)
                nc.tensor.matmul(out=l_sq_all[:], lhsT=ones[:], rhs=row_t[:], start=False, stop=True)
                first_path_step(LEAD + 1)
                logits_step(LEAD + 1)
                l_sq = early.tile([P, 1], F32)
                nc.vector.tensor_copy(out=l_sq[:], in_=l_sq_all[:])
                rough = early.tile([P, 1], F32)
                nc.scalar.activation(out=rough[:], in_=l_sq_all[:], func=ACT.Abs_reciprocal_sqrt)
                second_path_step(LEAD + 1)
                regroup_step(LEAD + 2)
                unit = early.tile([P, 1], F32)
                nc.vector.tensor_scalar(
                    out=unit[:],
                    in0=rough[:],
                    scalar1=l_sq[:, 0:1],
                    scalar2=rough[:, 0:1],
                    op0=ALU.mult,
                    op1=ALU.mult,
                )
                step_by = early.tile([P, 1], F32)
                nc.vector.tensor_scalar(
                    out=step_by[:], in0=unit[:], scalar1=-0.5, scalar2=1.5, op0=ALU.mult, op1=ALU.add
                )
                nc.vector.tensor_mul(out=l_inv[:], in0=rough[:], in1=step_by[:])

                for s in range(FIRST_CHUNK, GROUPS + 1):
                    if s > FIRST_CHUNK:
                        regroup_step(s)
                    c = s - FIRST_CHUNK
                    if c < PIECES:
                        scale_logits(c)
                    first_path_step(s)
                    if c < PIECES:
                        quantise_logits(c)
                    logits_step(s)
                    first_matmul_step(s)
                    second_path_step(s)
                    if s == FIRST_CHUNK:
                        nc.vector.tensor_scalar(
                            out=m_scale[:],
                            in0=l_inv[:],
                            scalar1=l_inv[:, 0:1],
                            scalar2=(ALPHA / KEEP) * (ALPHA / KEEP),
                            op0=ALU.mult,
                            op1=ALU.mult,
                        )

                first_matmul_step(GROUPS + 1)

                def keep_busy(count):
                    spare = psum.tile([P, R], F32, tag="bank", bufs=6)
                    for n in range(count):
                        nc.tensor.matmul_mx(
                            out=spare[:],
                            lhsT=l_codes[:, GROUPS - 1, :].bitcast(FP8X4),
                            lhsT_scale=l_scales[:, GROUPS - 1, :],
                            rhs=w0_codes[GROUPS - 1].bitcast(FP8X4),
                            rhs_scale=w0_scales[GROUPS - 1],
                            start=True,
                            stop=True,
                        )

                empty_banks(GROUPS - 1)
                quantise_by_r(GROUPS - 5)
                nc.vector.tensor_copy(
                    out=h_bf[:].rearrange("b (u e) q -> b u e q", e=2),
                    in_=h_acc[:].rearrange("b (u q e) -> b u e q", u=2, e=2),
                )
                keep_busy(2)
                h_t = psum.tile([P, PACK, P], BF16, tag="small")
                for t in range(PACK):
                    nc.tensor.transpose(out=h_t[:, t, :], in_=h_bf[:, t, :], identity=ident_bf[:])
                keep_busy(3)
                quantise_by_r(GROUPS - 4)
                nc.vector.tensor_copy(out=h_by_r[:], in_=h_t[:].rearrange("q t b -> q b t"))
                nc.vector.quantize_mx(
                    out=h_codes[:].bitcast(FP8X4),
                    scales=h_scales[:],
                    in_=h_by_r[:].rearrange("q b t -> q (b t)"),
                )
                quantise_by_r(GROUPS - 3)
                quantise_by_r(GROUPS - 2)
                quantise_by_r(GROUPS - 1)
                junk = stream.tile([P, R], BF16, tag="junk", bufs=2)
                nc.scalar.activation(
                    out=junk[:], in_=h_acc[:], func=ACT.Square, accum_out=h_sq[:, 0:1]
                )

                def minted_bank(g):
                    bank = psum.tile([P, K_PASS], F32, tag="bank", bufs=6)
                    nc.tensor.matmul_mx(
                        out=bank[:],
                        lhsT=h_codes[:].bitcast(FP8X4),
                        lhsT_scale=h_scales[:],
                        rhs=wt_codes[:, g, :].bitcast(FP8X4),
                        rhs_scale=wt_scales[:, g, :],
                        start=True,
                        stop=True,
                    )
                    return bank

                by_vector = sorted(list(range(1, GROUPS - 2, 2)) + [GROUPS // 2])
                by_scalar = [g for g in range(GROUPS) if g not in by_vector]
                for g in range(GROUPS):
                    bank = minted_bank(g)
                    if g in by_vector:
                        nc.vector.bn_stats(out=m_stats[:, by_vector.index(g), :], in_=bank[:])
                    else:
                        n = by_scalar.index(g)
                        junk = stream.tile([P, R], BF16, tag="junk", bufs=2)
                        nc.scalar.activation(
                            out=junk[:],
                            in_=bank[:],
                            func=ACT.Square,
                            accum_out=mm_parts[:, n : n + 1],
                        )
                    if g == 3:
                        h_sq_all = psum.tile([P, 1], F32, tag="small")
                        nc.tensor.matmul(
                            out=h_sq_all[:], lhsT=ones[:], rhs=h_sq[:], start=True, stop=True
                        )
                    if g == 5:
                        nc.vector.tensor_scalar(
                            out=dot_scale[:],
                            in0=h_sq_all[:],
                            scalar1=l_inv[:, 0:1],
                            scalar2=2.0,
                            op0=ALU.mult,
                            op1=ALU.mult,
                        )

        tail = ctx.enter_context(tc.tile_pool(name="tail", bufs=1, reuse_waits="tile"))
        ctx.enter_context(tc.manual_schedule())

        stores = [range(g, g + 1) for g in range(POST_SCALED)]
        stores += [range(g, g + 2) for g in range(POST_SCALED, GROUPS - 2, 2)]
        stores += [range(g, g + 1) for g in range(GROUPS - 2, GROUPS)]
        ahead = {}
        for k in range(POST_SCALED):
            for g in stores[k]:
                ahead[g] = minted_bank(g)

        m_mean_var = tail.tile([P, 2], F32)
        nc.vector.bn_aggr(out=m_mean_var[:], in_=m_stats[:].rearrange("p c s -> p (c s)"))
        m_mean_sq = tail.tile([P, 1], F32)
        nc.vector.scalar_tensor_tensor(
            out=m_mean_sq[:],
            in0=m_mean_var[:, 0:1],
            scalar=m_mean_var[:, 0:1],
            in1=m_mean_var[:, 1:2],
            op0=ALU.mult,
            op1=ALU.add,
        )
        nc.vector.tensor_scalar_mul(mm_v[:], m_mean_sq[:], float(V_SQUARES * K_PASS))
        nc.vector.tensor_reduce(out=mm_s[:], in_=mm_parts[:], axis=AXIS.X, op=ALU.add)
        mm_all = psum.tile([P, 1], F32, tag="small")
        nc.tensor.matmul(out=mm_all[:], lhsT=ones[:], rhs=mm_v[:], start=True, stop=False)
        nc.tensor.matmul(out=mm_all[:], lhsT=ones[:], rhs=mm_s[:], start=False, stop=True)
        ratio = tail.tile([P, 1], F32)
        nc.scalar.activation(
            out=ratio[:], in_=mm_all[:], func=ACT.Abs_reciprocal_sqrt, scale=m_scale[:, 0:1]
        )
        c_l = tail.tile([P, 1], F32)
        nc.scalar.activation(
            out=c_l[:],
            in_=ratio[:],
            func=ACT.Abs_reciprocal_sqrt,
            scale=dot_scale[:, 0:1],
            bias=o_const[:, 0:1],
        )
        c_m = tail.tile([P, 1], F32)

        def times_c_l(k, result, source):
            if k == POST_SCALED or (k > POST_SCALED and k % 3 == 2):
                nc.gpsimd.tensor_scalar(
                    out=result,
                    in0=source,
                    scalar1=c_l[:, 0:1],
                    scalar2=0.0,
                    op0=ALU.mult,
                    op1=ALU.add,
                )
            else:
                nc.scalar.activation(out=result, in_=source, func=ACT.Copy, scale=c_l[:, 0:1])

        results = {}

        def scale_ahead(k):
            width = len(stores[k]) * K_PASS
            g0 = stores[k][0]
            results[k] = tail.tile(
                [P, 2 * K_PASS], F32, tag="result", bufs=16, name="result"
            )
            if k >= POST_SCALED:
                times_c_l(
                    k, results[k][:, :width], logits_sb[:, g0 * K_PASS : g0 * K_PASS + width]
                )

        scale_ahead(0)
        scale_ahead(1)
        for k, groups in enumerate(stores):
            width = len(groups) * K_PASS
            cols = slice(groups[0] * K_PASS, groups[0] * K_PASS + width)
            if k + 2 < len(stores):
                scale_ahead(k + 2)
            result = results[k]
            for j, g in enumerate(groups):
                part = result[:, j * K_PASS : (j + 1) * K_PASS]
                bank = ahead[g] if g in ahead else minted_bank(g)
                if k < POST_SCALED:
                    term = logits_sb[:, g * K_PASS : (g + 1) * K_PASS]
                else:
                    term = part
                nc.vector.scalar_tensor_tensor(
                    out=part,
                    in0=bank[:],
                    scalar=ratio[:, 0:1] if k < POST_SCALED else c_m[:, 0:1],
                    in1=term,
                    op0=ALU.mult,
                    op1=ALU.add,
                )
            if k == 1:
                nc.vector.tensor_mul(out=c_m[:], in0=c_l[:], in1=ratio[:])
            if k < POST_SCALED:
                times_c_l(k, result[:, :width], result[:, :width])
            nc.sync.dma_start(out=out[:, cols], in_=result[:, :width])
